import numpy as np
import ml_dtypes


def mxq(x, axis, fmt="e4m3"):
    dtype, down = {"e4m3": (ml_dtypes.float8_e4m3fn, 7), "e5m2": (ml_dtypes.float8_e5m2, 14)}[fmt]
    v = np.moveaxis(np.asarray(x, np.float32).astype(ml_dtypes.bfloat16).astype(np.float64), axis, -1)
    blocks = v.reshape(v.shape[:-1] + (-1, 32))
    amax = np.abs(blocks).max(-1, keepdims=True)
    byte = np.maximum(np.where(amax > 0, np.frexp(amax)[1] - 1 + 127, 0) - down, 1)
    scale = np.exp2(byte - 127.0)
    codes = (blocks / scale).astype(np.float32).astype(dtype).astype(np.float64)
    return np.moveaxis((codes * scale).reshape(v.shape), -1, axis)


WIDE = False


def mx_kscale(k):
    if not WIDE:
        return np.ones(k)
    levels = np.array([10, -10, 5, -5, 0])
    a = np.random.permutation(np.resize(levels, k // 512 * 4)).reshape(k // 512, 4)
    idx = np.arange(k)
    return np.exp2(a[idx // 512, idx % 128 // 32])


BF16 = ml_dtypes.bfloat16


def bf(x):
    return np.asarray(x, np.float32).astype(BF16)


def f64(x):
    return np.asarray(x).astype(np.float64)


B, S, D_MODEL, N_HEADS, QK_ROPE, QK_NOPE, KV_LORA, V_DIM = 2, 256, 2048, 16, 128, 128, 512, 128
RMS_EPS = 1.1920928955078125e-07
ROPE_BASE = 10000.0


def apply_rope(r):
    freqs = 1.0 / (ROPE_BASE ** (np.arange(0, QK_ROPE, 2) / QK_ROPE))
    t = np.arange(S)[:, None] * freqs[None, :]
    cos = np.cos(t)[None, :, None, :]
    sin = np.sin(t)[None, :, None, :]
    r1 = r[..., 0::2]
    r2 = r[..., 1::2]
    return np.stack([r1 * cos - r2 * sin, r2 * cos + r1 * sin], axis=-1).reshape(r.shape)


def setup_inputs():
    s, t = mx_kscale(D_MODEL), mx_kscale(KV_LORA)
    return {"x": bf(np.random.standard_normal((B, S, D_MODEL)) * s),
            "Wkv_a": bf(np.random.standard_normal((D_MODEL, KV_LORA + QK_ROPE)) / np.sqrt(D_MODEL) / s[:, None]),
            "kv_norm_w": bf((1.0 + 0.1 * np.random.standard_normal(KV_LORA)) * t),
            "Wkv_b": bf(np.random.standard_normal((KV_LORA, N_HEADS * (QK_NOPE + V_DIM))) / np.sqrt(KV_LORA) / t[:, None])}


def reference(x, Wkv_a, kv_norm_w, Wkv_b):
    kv = mxq(f64(x), 2, "e4m3") @ mxq(f64(Wkv_a), 0, "e4m3")
    c_kv, k_rope = kv[..., :KV_LORA], kv[..., KV_LORA:]
    k_rope = apply_rope(k_rope.reshape(B, S, 1, QK_ROPE))
    c_kv = c_kv * (1.0 / np.sqrt(np.mean(c_kv * c_kv, axis=-1, keepdims=True) + RMS_EPS)) * f64(kv_norm_w)
    kv = (mxq(c_kv, 2, "e4m3") @ mxq(f64(Wkv_b), 0, "e4m3")).reshape(B, S, N_HEADS, QK_NOPE + V_DIM)
    return kv[..., :QK_NOPE], kv[..., QK_NOPE:], k_rope

@@ -1,0 +1,343 @@
+from contextlib import ExitStack
+
+import concourse.mybir as mybir
+from concourse.masks import make_identity
+
+F32 = mybir.dt.float32
+BF16 = mybir.dt.bfloat16
+I32 = mybir.dt.int32
+U32 = mybir.dt.uint32
+U8 = mybir.dt.uint8
+FP8X4 = mybir.dt.float8_e4m3fn_x4
+ALU = mybir.AluOpType
+ACT = mybir.ActivationFunctionType
+
+P = 128
+TOK = 512
+D_MODEL = 2048
+LORA = 512
+ROPE = 128
+A_COLS = LORA + ROPE
+KV_COLS = 4096
+RMS_EPS = 1.1920928955078125e-07
+ROPE_BASE = 10000.0
+TWO_PI = 6.283185307179586
+
+FLOPS = 2 * TOK * D_MODEL * A_COLS + 2 * TOK * LORA * KV_COLS
+
+WA_V_COLS = 320
+LOADS = (("Wa", 0), ("Wa", 1), ("Wa", 2), ("Wa", 3), ("w", 0), ("x", 0), ("x", 1), ("Wb", 0), ("x", 2), ("x", 3), ("Wb", 1), ("Wb", 2), ("Wb", 3))
+
+PLAN = (
+    ("Rs", 0), ("Rv", 0), ("Rs", 1), ("Rv", 1), ("Qc", 0), ("Qr", 0),
+    ("Rs", 2), ("Rv", 2), ("Qc", 1), ("Qr", 1), ("Rs", 3), ("G",),
+    ("Rv", 3), ("Gc",), ("TA", 0), ("Qc", 2), ("TB", 0), ("cA", 0, "S"),
+    ("Qc", 3), ("TA", 1), ("cB", 0, "S"), ("QA", 0), ("TB", 1), ("Qr", 2),
+    ("cA", 1, "S"), ("Qr", 3), ("QB", 0), ("cB", 1, "S"), ("QA", 1), ("M", 0),
+    ("QB", 1), ("WR", 0), ("M", 1), ("SQ", 0), ("WQ", 0), ("RT", 0),
+    ("TA", 2), ("SQ", 1), ("RC", 0), ("NM", 0), ("TB", 2), ("TA", 3),
+    ("RT", 1), ("WR", 1), ("N", 0), ("cA", 2, "S"), ("TB", 3), ("RP", 0),
+    ("cN", 0, "S"), ("RP", 1), ("RC", 1), ("NM", 1), ("cB", 2, "S"), ("QN", 0),
+    ("cA", 3, "S"), ("N", 1), ("QA", 2), ("QB", 2), ("P", 0, 0), ("cB", 3, "S"),
+    ("cN", 1, "V"), ("M", 2), ("d", 0, 0, "S"), ("QN", 1), ("QA", 3), ("QB", 3),
+    ("WQ", 1), ("P", 1, 0), ("SQ", 2), ("M", 3), ("WR", 2), ("d", 1, 0, "S"),
+    ("P", 0, 1), ("RT", 2), ("WQ", 2), ("P", 1, 1), ("SQ", 3), ("RP", 2),
+    ("RC", 2), ("RP", 3), ("NM", 2), ("d", 0, 1, "S"), ("P", 0, 2), ("P", 1, 2),
+    ("ro", 1), ("RT", 3), ("N", 2), ("d", 1, 1, "S"), ("RC", 3), ("NM", 3),
+    ("cN", 2, "S"), ("ro", 2), ("N", 3), ("d", 0, 2, "S"), ("ro", 3), ("QN", 2),
+    ("cN", 3, "S"), ("ro", 4), ("P", 2, 0), ("d", 1, 2, "S"), ("WR", 3), ("P", 2, 1),
+    ("P", 2, 2), ("d", 2, 0, "S"), ("d", 2, 1, "S"), ("QN", 3), ("WQ", 3), ("d", 2, 2, "S"),
+    ("P", 3, 0), ("WR", 4), ("P", 3, 1), ("d", 3, 0, "S"), ("P", 3, 2), ("P", 0, 3),
+    ("P", 1, 3), ("d", 3, 1, "S"), ("WQ", 4), ("P", 2, 3), ("P", 3, 3), ("d", 3, 2, "S"),
+    ("WR", 5), ("d", 0, 3, "S"), ("P", 0, 4), ("P", 1, 4), ("P", 2, 4), ("d", 1, 3, "S"),
+    ("WQ", 5), ("P", 3, 4), ("d", 2, 3, "S"), ("WR", 6), ("d", 3, 3, "S"), ("P", 0, 5),
+    ("P", 1, 5), ("P", 2, 5), ("d", 0, 4, "S"), ("WQ", 6), ("P", 3, 5), ("d", 1, 4, "S"),
+    ("WR", 7), ("P", 0, 6), ("d", 2, 4, "S"), ("P", 1, 6), ("d", 3, 4, "S"), ("d", 3, 5, "V"),
+    ("P", 2, 6), ("d", 0, 5, "S"), ("WQ", 7), ("P", 3, 6), ("d", 1, 5, "S"), ("d", 3, 6, "V"),
+    ("d", 2, 5, "S"), ("P", 0, 7), ("P", 1, 7), ("P", 2, 7), ("d", 0, 6, "S"), ("d", 1, 7, "V"),
+    ("P", 3, 7), ("d", 1, 6, "S"), ("d", 3, 7, "V"), ("d", 2, 6, "S"), ("d", 0, 7, "S"), ("d", 2, 7, "S"),
+)
+
+
+def tile_multiheadlatentattention_pa_kernel(tc, x, Wkv_a, kv_norm_w, Wkv_b, out_0, out_1, out_2):
+    nc = tc.nc
+    xf = x.flatten_outer_dims()
+    outs = [
+        out_0.rearrange("b s h d -> (b s) (h d)"),
+        out_1.rearrange("b s h d -> (b s) (h d)"),
+    ]
+    with ExitStack() as ctx:
+        keep = ctx.enter_context(tc.tile_pool(name="keep", bufs=1))
+        stage = ctx.enter_context(tc.tile_pool(name="stage", bufs=4))
+        outp = ctx.enter_context(tc.tile_pool(name="outp", bufs=12))
+        psum = ctx.enter_context(tc.psum_pool(name="psum", bufs=7))
+        psr = ctx.enter_context(tc.psum_pool(name="psr", bufs=1))
+        ctx.enter_context(tc.manual_schedule())
+
+        wrow = keep.tile([P, LORA], BF16, name="wrow")
+        nc.vector.memset(wrow[:], 0.0)
+        pos_i = keep.tile([P, 2], I32, name="pos_i")
+        nc.gpsimd.iota(pos_i[:], pattern=[[P, 2]], base=0, channel_multiplier=1)
+
+        wa_raw = [keep.tile([P, 4, A_COLS], BF16, name="wa_raw%d" % g) for g in range(4)]
+        x_raw = [keep.tile([P, D_MODEL], BF16, name="x_raw%d" % a) for a in range(4)]
+        wb_raw = [keep.tile([P, 4, 1024], BF16, name="wb_raw%d" % c) for c in range(4)]
+        for what, i in LOADS:
+            if what == "Wa":
+                nc.sync.dma_start(
+                    out=wa_raw[i][:].rearrange("p (u e) c -> p u (e c)", u=2, e=2),
+                    in_=Wkv_a[512 * i : 512 * (i + 1), :].rearrange("(u p e) c -> p u (e c)", u=2, p=P, e=2),
+                )
+            elif what == "x":
+                nc.sync.dma_start(out=x_raw[i][:], in_=xf[P * i : P * (i + 1), :])
+            elif what == "Wb":
+                nc.sync.dma_start(
+                    out=wb_raw[i][:],
+                    in_=Wkv_b[:, 1024 * i : 1024 * (i + 1)].rearrange("(t p) n -> p t n", t=4, p=P),
+                )
+            else:
+                nc.sync.dma_start(out=wrow[0:1, :], in_=kv_norm_w.rearrange("(o n) -> o n", o=1))
+
+        freq = keep.tile([P, 64], F32, name="freq")
+        nc.vector.memset(freq[:, 0:1], 1.0)
+        for j in range(6):
+            w = 2 ** j
+            nc.vector.tensor_scalar_mul(
+                out=freq[:, w : 2 * w], in0=freq[:, 0:w], scalar1=ROPE_BASE ** (-2.0 * w / ROPE)
+            )
+        pos_f = keep.tile([P, 2], F32, name="pos_f")
+        nc.vector.tensor_copy(out=pos_f[:], in_=pos_i[:])
+        turns = keep.tile([P, 2, 2, 64], F32, name="turns")
+        for h in range(2):
+            nc.vector.tensor_scalar(
+                out=turns[:, 0, h, :], in0=freq[:], scalar1=pos_f[:, h : h + 1], scalar2=1.0 / TWO_PI,
+                op0=ALU.mult, op1=ALU.mult,
+            )
+        nc.vector.tensor_scalar_add(out=turns[:, 1, :, :], in0=turns[:, 0, :, :], scalar1=0.25)
+        turns_flat = turns[:].rearrange("p s h i -> p (s h i)")
+        whole_i = keep.tile([P, 256], I32, name="whole_i")
+        nc.vector.tensor_copy(out=whole_i[:], in_=turns_flat)
+        whole_f = keep.tile([P, 256], F32, name="whole_f")
+        nc.vector.tensor_copy(out=whole_f[:], in_=whole_i[:])
+        frac = keep.tile([P, 256], F32, name="frac")
+        nc.vector.tensor_tensor(out=frac[:], in0=turns_flat, in1=whole_f[:], op=ALU.subtract)
+        trig = keep.tile([P, 3, P], F32, name="trig")
+        nc.scalar.activation(
+            out=trig[:, 0:2, :].rearrange("p s n -> p (s n)"), in_=frac[:], func=ACT.Sin, scale=TWO_PI
+        )
+        nc.scalar.activation(out=trig[:, 2, :], in_=frac[:, 0:P], func=ACT.Sin, scale=-TWO_PI)
+        eps_t = keep.tile([P, 1], F32, name="eps_t")
+        nc.vector.memset(eps_t[:], RMS_EPS)
+        warm = keep.tile([P, 1], F32, name="warm")
+        nc.scalar.activation(out=warm[:], in_=eps_t[:], func=ACT.Sqrt)
+        ones = keep.tile([P, P], BF16, name="ones")
+        nc.vector.memset(ones[:], 1.0)
+        ident_f = keep.tile([P, P], F32, name="ident_f")
+        make_identity(nc, ident_f[:])
+        ident_b = keep.tile([P, P], BF16, name="ident_b")
+        make_identity(nc, ident_b[:])
+
+        gain = keep.tile([P, LORA], F32, name="gain")
+        wa_codes = keep.tile([P, 4, A_COLS], U32, name="wa_codes", align_bytes=64)
+        wa_scales = keep.tile([P, 4, A_COLS], U8, name="wa_scales", align_bytes=64)
+        x_codes = [keep.tile([P, 512], U32, name="x_codes%d" % a, align_bytes=64) for a in range(4)]
+        x_scales = [keep.tile([P, 512], U8, name="x_scales%d" % a, align_bytes=64) for a in range(4)]
+        n_codes = [keep.tile([P, P], U32, name="n_codes%d" % a, align_bytes=64) for a in range(4)]
+        n_scales = [keep.tile([P, P], U8, name="n_scales%d" % a, align_bytes=64) for a in range(4)]
+        sumsq = [keep.tile([P, 1], F32, name="sumsq%d" % a) for a in range(4)]
+        rms = [keep.tile([P, 1], F32, name="rms%d" % a) for a in range(4)]
+        rstd = [keep.tile([P, 1], F32, name="rstd%d" % a) for a in range(4)]
+        wb_codes = keep.tile([P, 8, 512], U32, name="wb_codes", align_bytes=64)
+        wb_scales = keep.tile([P, 8, 512], U8, name="wb_scales", align_bytes=64)
+        rope_ps = psr.tile([P, 4, ROPE], F32, name="rope_ps")
+        straight = keep.tile([P, 2, P, 2], F32, name="straight")
+        crossed = keep.tile([P, 2, 2, P], F32, name="crossed")
+        turned = keep.tile([P, 2, P, 2], F32, name="turned")
+        live = {}
+
+        def copy_on(engine, out, in_):
+            if engine == "V":
+                nc.vector.tensor_copy(out=out, in_=in_)
+            else:
+                nc.scalar.copy(out=out, in_=in_)
+
+        def wa_regroup(g, engine, c0, c1):
+            if ("ga", g) not in live:
+                live[("ga", g)] = stage.tile([P, A_COLS, 4], BF16, name="ga", tag="ga", align_bytes=64)
+            copy_on(
+                engine,
+                live[("ga", g)][:, c0:c1, :].rearrange("p (c i) t -> p c t i", i=4),
+                wa_raw[g][:, :, c0:c1].rearrange("p t (c i) -> p c t i", i=4),
+            )
+
+        def wa_quantise(g, c0, c1):
+            nc.vector.quantize_mx(
+                out=wa_codes[:, g, c0:c1].bitcast(FP8X4),
+                scales=wa_scales[:, g, c0:c1],
+                in_=live[("ga", g)][:, c0:c1, :].rearrange("p c t -> p (c t)"),
+            )
+
+        def x_transpose(a, b):
+            words = x_raw[a][:].bitcast(F32)
+            xt = psum.tile([P, 2, 2, P], F32, name="xt", tag="ps")
+            live[("xt", a, b)] = xt
+            for gg in range(2):
+                for u in range(2):
+                    w0 = 256 * (2 * b + gg) + P * u
+                    nc.tensor.transpose(xt[:, gg, u, :], words[:, w0 : w0 + P], ident_f[:])
+
+        def x_copy(a, b, engine):
+            if ("gx", a) not in live:
+                live[("gx", a)] = stage.tile([P, 4, P, 2], F32, name="gx", tag="gx", align_bytes=64)
+            copy_on(
+                engine,
+                live[("gx", a)][:, 2 * b : 2 * b + 2, :, :],
+                live[("xt", a, b)][:].rearrange("p g u r -> p g r u"),
+            )
+
+        def x_quantise(a, b):
+            nc.vector.quantize_mx(
+                out=x_codes[a][:, 256 * b : 256 * (b + 1)].bitcast(FP8X4),
+                scales=x_scales[a][:, 256 * b : 256 * (b + 1)],
+                in_=live[("gx", a)][:, 2 * b : 2 * b + 2, :, :].rearrange("p g r u -> p (g r u)").bitcast(BF16),
+            )
+
+        def first_matmul(a, dst, c0, c1):
+            for g in range(4):
+                nc.tensor.matmul_mx(
+                    out=dst,
+                    lhsT=x_codes[a][:, P * g : P * (g + 1)].bitcast(FP8X4),
+                    lhsT_scale=x_scales[a][:, P * g : P * (g + 1)],
+                    rhs=wa_codes[:, g, c0:c1].bitcast(FP8X4),
+                    rhs_scale=wa_scales[:, g, c0:c1],
+                    start=(g == 0),
+                    stop=(g == 3),
+                )
+
+        def wb_regroup(j):
+            cc, kv = j // 2, j % 2
+            t = stage.tile([P, 512, 4], BF16, name="gb", tag="gb", align_bytes=64)
+            live[("gb", j)] = t
+            src = wb_raw[cc][:].rearrange("p t (h k c i) -> p t h k c i", h=4, k=2, c=32, i=4)
+            nc.vector.tensor_copy(
+                out=t[:].rearrange("p (h c i) t -> p h c t i", h=4, c=32, i=4),
+                in_=src[:, :, :, kv, :, :].rearrange("p t h c i -> p h c t i"),
+            )
+
+        r4 = rope_ps[:].rearrange("p (b h) (i e) -> p b (h i) e", b=2, e=2)
+
+        def emit(op):
+            kind = op[0]
+            if kind == "G":
+                live["gain_ps"] = psum.tile([P, LORA], F32, name="gain_ps", tag="ps")
+                nc.tensor.matmul(out=live["gain_ps"][:], lhsT=ones[:], rhs=wrow[:], start=True, stop=True)
+            elif kind == "Gc":
+                nc.vector.tensor_copy(out=gain[:], in_=live["gain_ps"][:])
+            elif kind == "Rv":
+                wa_regroup(op[1], "V", 0, WA_V_COLS)
+            elif kind == "Rs":
+                wa_regroup(op[1], "S", WA_V_COLS, A_COLS)
+            elif kind == "Qc":
+                wa_quantise(op[1], 0, LORA)
+            elif kind == "Qr":
+                wa_quantise(op[1], LORA, A_COLS)
+            elif kind == "TA":
+                x_transpose(op[1], 0)
+            elif kind == "TB":
+                x_transpose(op[1], 1)
+            elif kind == "cA":
+                x_copy(op[1], 0, op[2])
+            elif kind == "cB":
+                x_copy(op[1], 1, op[2])
+            elif kind == "QA":
+                x_quantise(op[1], 0)
+            elif kind == "QB":
+                x_quantise(op[1], 1)
+            elif kind == "M":
+                live[("c", op[1])] = psum.tile([P, LORA], F32, name="c_ps", tag="ps")
+                first_matmul(op[1], live[("c", op[1])][:], 0, LORA)
+            elif kind == "RP":
+                first_matmul(op[1], rope_ps[:, op[1], :], LORA, A_COLS)
+            elif kind == "SQ":
+                junk = stage.tile([P, LORA], BF16, name="junk", tag="junk")
+                nc.scalar.activation(out=junk[:], in_=live[("c", op[1])][:], func=ACT.Square, accum_out=sumsq[op[1]][:])
+            elif kind == "RT":
+                nc.scalar.activation(
+                    out=rms[op[1]][:], in_=sumsq[op[1]][:], func=ACT.Sqrt, scale=1.0 / LORA, bias=eps_t[:]
+                )
+            elif kind == "RC":
+                nc.vector.reciprocal(out=rstd[op[1]][:], in_=rms[op[1]][:])
+            elif kind == "NM":
+                live[("n", op[1])] = stage.tile([P, LORA], BF16, name="n_bf", tag="n_bf")
+                nc.vector.scalar_tensor_tensor(
+                    out=live[("n", op[1])][:], in0=live[("c", op[1])][:], scalar=rstd[op[1]][:], in1=gain[:],
+                    op0=ALU.mult, op1=ALU.mult,
+                )
+            elif kind == "N":
+                nt = psum.tile([P, 4, P], BF16, name="nt", tag="ps")
+                live[("nt", op[1])] = nt
+                for t in range(4):
+                    nc.tensor.transpose(nt[:, t, :], live[("n", op[1])][:, P * t : P * (t + 1)], ident_b[:])
+            elif kind == "cN":
+                live[("gn", op[1])] = stage.tile([P, P, 4], BF16, name="gn", tag="gn", align_bytes=64)
+                copy_on(op[2], live[("gn", op[1])][:], live[("nt", op[1])][:].rearrange("p t r -> p r t"))
+            elif kind == "QN":
+                nc.vector.quantize_mx(
+                    out=n_codes[op[1]][:].bitcast(FP8X4),
+                    scales=n_scales[op[1]][:],
+                    in_=live[("gn", op[1])][:].rearrange("p r t -> p (r t)"),
+                )
+            elif kind == "WR":
+                wb_regroup(op[1])
+            elif kind == "WQ":
+                nc.vector.quantize_mx(
+                    out=wb_codes[:, op[1], :].bitcast(FP8X4),
+                    scales=wb_scales[:, op[1], :],
+                    in_=live[("gb", op[1])][:].rearrange("p c t -> p (c t)"),
+                )
+            elif kind == "P":
+                a, j = op[1], op[2]
+                live[("o", a, j)] = psum.tile([P, 512], F32, name="o_ps", tag="ps")
+                nc.tensor.matmul_mx(
+                    out=live[("o", a, j)][:],
+                    lhsT=n_codes[a][:].bitcast(FP8X4),
+                    lhsT_scale=n_scales[a][:],
+                    rhs=wb_codes[:, j, :].bitcast(FP8X4),
+                    rhs_scale=wb_scales[:, j, :],
+                    start=True,
+                    stop=True,
+                )
+            elif kind == "d":
+                a, j = op[1], op[2]
+                st = outp.tile([P, 512], F32, name="st", tag="st")
+                copy_on(op[3], st[:], live[("o", a, j)][:])
+                nc.sync.dma_start(
+                    out=outs[j % 2][P * a : P * (a + 1), 512 * (j // 2) : 512 * (j // 2 + 1)], in_=st[:]
+                )
+            elif kind == "ro":
+                if op[1] == 1:
+                    nc.vector.tensor_tensor(
+                        out=straight[:], in0=r4,
+                        in1=trig[:, 1, :].unsqueeze(1).unsqueeze(3).to_broadcast([P, 2, P, 2]), op=ALU.mult,
+                    )
+                elif op[1] == 2:
+                    nc.vector.tensor_tensor(
+                        out=crossed[:, 0, :, :], in0=r4[:, :, :, 1],
+                        in1=trig[:, 2, :].unsqueeze(1).to_broadcast([P, 2, P]), op=ALU.mult,
+                    )
+                elif op[1] == 3:
+                    nc.vector.tensor_tensor(
+                        out=crossed[:, 1, :, :], in0=r4[:, :, :, 0],
+                        in1=trig[:, 0, :].unsqueeze(1).to_broadcast([P, 2, P]), op=ALU.mult,
+                    )
+                else:
+                    nc.vector.tensor_tensor(
+                        out=turned[:], in0=straight[:], in1=crossed[:].rearrange("p e b n -> p b n e"), op=ALU.add
+                    )
+                    nc.sync.dma_start(
+                        out=out_2.rearrange("b (h p) o d -> p (b h) (o d)", h=2, p=P),
+                        in_=turned[:].rearrange("p b (h i) e -> p (b h) (i e)", h=2),
+                    )
+
+        for op in PLAN:
+            emit(op)

@@ -29,11 +29,11 @@ WA_V_COLS = 320
 LOADS = (("Wa", 0), ("Wa", 1), ("Wa", 2), ("Wa", 3), ("w", 0), ("x", 0), ("x", 1), ("Wb", 0), ("x", 2), ("x", 3), ("Wb", 1), ("Wb", 2), ("Wb", 3))
 
 PLAN = (
-    ("Rs", 0), ("Rv", 0), ("Rs", 1), ("Rv", 1), ("Qc", 0), ("Qr", 0),
+    ("Rs", 0), ("Sin",), ("Rv", 0), ("Rs", 1), ("Rv", 1), ("Qc", 0), ("Qr", 0),
     ("Rs", 2), ("Rv", 2), ("Qc", 1), ("Qr", 1), ("Rs", 3), ("G",),
     ("Rv", 3), ("Gc",), ("TA", 0), ("Qc", 2), ("TB", 0), ("cA", 0, "S"),
     ("Qc", 3), ("TA", 1), ("cB", 0, "S"), ("QA", 0), ("TB", 1), ("Qr", 2),
-    ("cA", 1, "S"), ("Qr", 3), ("QB", 0), ("cB", 1, "S"), ("QA", 1), ("M", 0),
+    ("cA", 1, "S"), ("Qr", 3), ("QB", 0), ("cB", 1, "S"), ("Wm",), ("QA", 1), ("M", 0),
     ("QB", 1), ("WR", 0), ("M", 1), ("SQ", 0), ("WQ", 0), ("RT", 0),
     ("TA", 2), ("SQ", 1), ("RC", 0), ("NM", 0), ("TB", 2), ("TA", 3),
     ("RT", 1), ("WR", 1), ("N", 0), ("cA", 2, "S"), ("TB", 3), ("RP", 0),
@@ -74,6 +74,10 @@ def tile_multiheadlatentattention_pa_kernel(tc, x, Wkv_a, kv_norm_w, Wkv_b, out_
         psr = ctx.enter_context(tc.psum_pool(name="psr", bufs=1))
         ctx.enter_context(tc.manual_schedule())
 
+        eps_t = keep.tile([P, 1], F32, name="eps_t")
+        nc.vector.memset(eps_t[:], RMS_EPS)
+        warm = keep.tile([P, 2], F32, name="warm")
+        nc.scalar.activation(out=warm[:, 0:1], in_=eps_t[:], func=ACT.Sin)
         wrow = keep.tile([P, LORA], BF16, name="wrow")
         nc.vector.memset(wrow[:], 0.0)
         pos_i = keep.tile([P, 2], I32, name="pos_i")
@@ -122,14 +126,6 @@ def tile_multiheadlatentattention_pa_kernel(tc, x, Wkv_a, kv_norm_w, Wkv_b, out_
         frac = keep.tile([P, 256], F32, name="frac")
         nc.vector.tensor_tensor(out=frac[:], in0=turns_flat, in1=whole_f[:], op=ALU.subtract)
         trig = keep.tile([P, 3, P], F32, name="trig")
-        nc.scalar.activation(
-            out=trig[:, 0:2, :].rearrange("p s n -> p (s n)"), in_=frac[:], func=ACT.Sin, scale=TWO_PI
-        )
-        nc.scalar.activation(out=trig[:, 2, :], in_=frac[:, 0:P], func=ACT.Sin, scale=-TWO_PI)
-        eps_t = keep.tile([P, 1], F32, name="eps_t")
-        nc.vector.memset(eps_t[:], RMS_EPS)
-        warm = keep.tile([P, 1], F32, name="warm")
-        nc.scalar.activation(out=warm[:], in_=eps_t[:], func=ACT.Sqrt)
         ones = keep.tile([P, P], BF16, name="ones")
         nc.vector.memset(ones[:], 1.0)
         ident_f = keep.tile([P, P], F32, name="ident_f")
@@ -231,6 +227,13 @@ def tile_multiheadlatentattention_pa_kernel(tc, x, Wkv_a, kv_norm_w, Wkv_b, out_
             if kind == "G":
                 live["gain_ps"] = psum.tile([P, LORA], F32, name="gain_ps", tag="ps")
                 nc.tensor.matmul(out=live["gain_ps"][:], lhsT=ones[:], rhs=wrow[:], start=True, stop=True)
+            elif kind == "Sin":
+                nc.scalar.activation(
+                    out=trig[:, 0:2, :].rearrange("p s n -> p (s n)"), in_=frac[:], func=ACT.Sin, scale=TWO_PI
+                )
+                nc.scalar.activation(out=trig[:, 2, :], in_=frac[:, 0:P], func=ACT.Sin, scale=-TWO_PI)
+            elif kind == "Wm":
+                nc.scalar.activation(out=warm[:, 1:2], in_=eps_t[:], func=ACT.Sqrt)
             elif kind == "Gc":
                 nc.vector.tensor_copy(out=gain[:], in_=live["gain_ps"][:])
             elif kind == "Rv":

@@ -25,37 +25,39 @@ TWO_PI = 6.283185307179586
 
 FLOPS = 2 * TOK * D_MODEL * A_COLS + 2 * TOK * LORA * KV_COLS
 
+WB_LOAD = ((0, 1), (1, 2), (3, 1))
+PIECE = ((0, 0), (0, 1), (1, 0), (2, 0), (1, 1), (2, 1), (3, 0), (3, 1))
 WA_V_COLS = 320
-LOADS = (("Wa", 0), ("Wa", 1), ("Wa", 2), ("Wa", 3), ("w", 0), ("x", 0), ("x", 1), ("Wb", 0), ("x", 2), ("x", 3), ("Wb", 1), ("Wb", 2), ("Wb", 3))
+LOADS = (("Wa", 0), ("Wa", 1), ("Wa", 2), ("Wa", 3), ("w", 0), ("x", 0), ("x", 1), ("Wb", 0), ("x", 2), ("x", 3), ("Wb", 1), ("Wb", 2))
 
 PLAN = (
-    ("Rs", 0), ("Sin",), ("Rv", 0), ("Rs", 1), ("Rv", 1), ("Qc", 0), ("Qr", 0),
-    ("Rs", 2), ("Rv", 2), ("Qc", 1), ("Qr", 1), ("Rs", 3), ("G",),
-    ("Rv", 3), ("Gc",), ("TA", 0), ("Qc", 2), ("TB", 0), ("cA", 0, "S"),
-    ("Qc", 3), ("TA", 1), ("cB", 0, "S"), ("QA", 0), ("TB", 1), ("Qr", 2),
-    ("cA", 1, "S"), ("Qr", 3), ("QB", 0), ("cB", 1, "S"), ("Wm",), ("QA", 1), ("M", 0),
-    ("QB", 1), ("WR", 0), ("M", 1), ("SQ", 0), ("WQ", 0), ("RT", 0),
-    ("TA", 2), ("SQ", 1), ("RC", 0), ("NM", 0), ("TB", 2), ("TA", 3),
-    ("RT", 1), ("WR", 1), ("N", 0), ("cA", 2, "S"), ("TB", 3), ("RP", 0),
-    ("cN", 0, "S"), ("RP", 1), ("RC", 1), ("NM", 1), ("cB", 2, "S"), ("QN", 0),
-    ("cA", 3, "S"), ("N", 1), ("QA", 2), ("QB", 2), ("P", 0, 0), ("cB", 3, "S"),
-    ("cN", 1, "V"), ("M", 2), ("d", 0, 0, "S"), ("QN", 1), ("QA", 3), ("QB", 3),
-    ("WQ", 1), ("P", 1, 0), ("SQ", 2), ("M", 3), ("WR", 2), ("d", 1, 0, "S"),
-    ("P", 0, 1), ("RT", 2), ("WQ", 2), ("P", 1, 1), ("SQ", 3), ("RP", 2),
-    ("RC", 2), ("RP", 3), ("NM", 2), ("d", 0, 1, "S"), ("P", 0, 2), ("P", 1, 2),
-    ("ro", 1), ("RT", 3), ("N", 2), ("d", 1, 1, "S"), ("RC", 3), ("NM", 3),
-    ("cN", 2, "S"), ("ro", 2), ("N", 3), ("d", 0, 2, "S"), ("ro", 3), ("QN", 2),
-    ("cN", 3, "S"), ("ro", 4), ("P", 2, 0), ("d", 1, 2, "S"), ("WR", 3), ("P", 2, 1),
-    ("P", 2, 2), ("d", 2, 0, "S"), ("d", 2, 1, "S"), ("QN", 3), ("WQ", 3), ("d", 2, 2, "S"),
-    ("P", 3, 0), ("WR", 4), ("P", 3, 1), ("d", 3, 0, "S"), ("P", 3, 2), ("P", 0, 3),
-    ("P", 1, 3), ("d", 3, 1, "S"), ("WQ", 4), ("P", 2, 3), ("P", 3, 3), ("d", 3, 2, "S"),
-    ("WR", 5), ("d", 0, 3, "S"), ("P", 0, 4), ("P", 1, 4), ("P", 2, 4), ("d", 1, 3, "S"),
-    ("WQ", 5), ("P", 3, 4), ("d", 2, 3, "S"), ("WR", 6), ("d", 3, 3, "S"), ("P", 0, 5),
-    ("P", 1, 5), ("P", 2, 5), ("d", 0, 4, "S"), ("WQ", 6), ("P", 3, 5), ("d", 1, 4, "S"),
-    ("WR", 7), ("P", 0, 6), ("d", 2, 4, "S"), ("P", 1, 6), ("d", 3, 4, "S"), ("d", 3, 5, "V"),
-    ("P", 2, 6), ("d", 0, 5, "S"), ("WQ", 7), ("P", 3, 6), ("d", 1, 5, "S"), ("d", 3, 6, "V"),
-    ("d", 2, 5, "S"), ("P", 0, 7), ("P", 1, 7), ("P", 2, 7), ("d", 0, 6, "S"), ("d", 1, 7, "V"),
-    ("P", 3, 7), ("d", 1, 6, "S"), ("d", 3, 7, "V"), ("d", 2, 6, "S"), ("d", 0, 7, "S"), ("d", 2, 7, "S"),
+    ("Rs", 0), ("Rv", 0), ("Sin",), ("Rv", 1), ("Rs", 1), ("Qc", 0),
+    ("Qr", 0), ("Rv", 2), ("Rs", 2), ("Qc", 1), ("G",), ("Rv", 3),
+    ("Rs", 3), ("Gc",), ("TA", 0), ("TB", 0), ("Qc", 2), ("cA", 0, "S"),
+    ("Qc", 3), ("TA", 1), ("cB", 0, "S"), ("TB", 1), ("cA", 1, "S"), ("Q", 0),
+    ("cB", 1, "S"), ("Qr", 1), ("M", 0), ("Wm",), ("Qr", 2), ("Q", 1),
+    ("Qr", 3), ("WR", 0), ("M", 1), ("SQ", 0), ("WQ", 0), ("RT", 0),
+    ("TA", 2), ("SQ", 1), ("WR", 1), ("TB", 2), ("TA", 3), ("RT", 1),
+    ("TB", 3), ("cA", 2, "S"), ("RP", 0), ("RC", 0), ("cB", 2, "S"), ("NM", 0),
+    ("RP", 1), ("cA", 3, "S"), ("RC", 1), ("NM", 1), ("N", 0), ("cB", 3, "S"),
+    ("N", 1), ("cN", 0, "S"), ("Q", 2), ("cN", 1, "S"), ("QN", 0), ("M", 2),
+    ("Q", 3), ("QN", 1), ("WQ", 1), ("P", 0, 0), ("WR", 2), ("SQ", 2),
+    ("P", 1, 0), ("P", 0, 1), ("M", 3), ("d", 0, 0, "S"), ("WQ", 2), ("d", 1, 0, "S"),
+    ("WR", 3), ("P", 1, 1), ("RT", 2), ("d", 0, 1, "S"), ("RP", 2), ("P", 0, 2),
+    ("SQ", 3), ("P", 1, 2), ("RP", 3), ("RC", 2), ("NM", 2), ("RT", 3),
+    ("d", 1, 1, "S"), ("RC", 3), ("NM", 3), ("N", 2), ("d", 0, 2, "S"), ("WQ", 3),
+    ("cN", 2, "S"), ("N", 3), ("cN", 3, "S"), ("WR", 4), ("P", 0, 3), ("d", 1, 2, "S"),
+    ("P", 1, 3), ("d", 0, 3, "S"), ("QN", 2), ("QN", 3), ("WQ", 4), ("d", 1, 3, "S"),
+    ("P", 2, 0), ("P", 3, 0), ("WR", 5), ("d", 2, 0, "S"), ("P", 2, 1), ("P", 3, 1),
+    ("d", 3, 0, "S"), ("P", 2, 2), ("P", 3, 2), ("d", 2, 1, "S"), ("P", 2, 3), ("WQ", 5),
+    ("ro", 1), ("ro", 2), ("ro", 3), ("ro", 4), ("P", 3, 3), ("d", 3, 1, "S"),
+    ("P", 0, 4), ("WR", 6), ("P", 1, 4), ("d", 2, 2, "S"), ("P", 2, 4), ("P", 3, 4),
+    ("d", 3, 2, "S"), ("WQ", 6), ("P", 0, 5), ("d", 2, 3, "S"), ("d", 3, 4, "V"), ("P", 1, 5),
+    ("d", 3, 3, "S"), ("P", 2, 5), ("WR", 7), ("d", 0, 4, "S"), ("P", 3, 5), ("P", 0, 6),
+    ("d", 1, 4, "S"), ("P", 1, 6), ("d", 2, 4, "S"), ("d", 3, 5, "V"), ("P", 2, 6), ("d", 0, 5, "S"),
+    ("WQ", 7), ("P", 3, 6), ("d", 1, 5, "S"), ("d", 3, 6, "V"), ("d", 2, 5, "S"), ("P", 0, 7),
+    ("P", 1, 7), ("d", 0, 6, "S"), ("P", 2, 7), ("P", 3, 7), ("d", 1, 7, "V"), ("d", 1, 6, "S"),
+    ("d", 2, 6, "S"), ("d", 3, 7, "V"), ("d", 0, 7, "S"), ("d", 2, 7, "S"),
 )
 
 
@@ -69,7 +71,7 @@ def tile_multiheadlatentattention_pa_kernel(tc, x, Wkv_a, kv_norm_w, Wkv_b, out_
     with ExitStack() as ctx:
         keep = ctx.enter_context(tc.tile_pool(name="keep", bufs=1))
         stage = ctx.enter_context(tc.tile_pool(name="stage", bufs=4))
-        outp = ctx.enter_context(tc.tile_pool(name="outp", bufs=12))
+        outp = ctx.enter_context(tc.tile_pool(name="outp", bufs=8))
         psum = ctx.enter_context(tc.psum_pool(name="psum", bufs=7))
         psr = ctx.enter_context(tc.psum_pool(name="psr", bufs=1))
         ctx.enter_context(tc.manual_schedule())
@@ -85,7 +87,7 @@ def tile_multiheadlatentattention_pa_kernel(tc, x, Wkv_a, kv_norm_w, Wkv_b, out_
 
         wa_raw = [keep.tile([P, 4, A_COLS], BF16, name="wa_raw%d" % g) for g in range(4)]
         x_raw = [keep.tile([P, D_MODEL], BF16, name="x_raw%d" % a) for a in range(4)]
-        wb_raw = [keep.tile([P, 4, 1024], BF16, name="wb_raw%d" % c) for c in range(4)]
+        wb_raw = [keep.tile([P, 4, 1024 * WB_LOAD[c][1]], BF16, name="wb_raw%d" % c) for c in range(3)]
         for what, i in LOADS:
             if what == "Wa":
                 nc.sync.dma_start(
@@ -97,7 +99,9 @@ def tile_multiheadlatentattention_pa_kernel(tc, x, Wkv_a, kv_norm_w, Wkv_b, out_
             elif what == "Wb":
                 nc.sync.dma_start(
                     out=wb_raw[i][:],
-                    in_=Wkv_b[:, 1024 * i : 1024 * (i + 1)].rearrange("(t p) n -> p t n", t=4, p=P),
+                    in_=Wkv_b[:, 1024 * WB_LOAD[i][0] : 1024 * (WB_LOAD[i][0] + WB_LOAD[i][1])].rearrange(
+                        "(t p) n -> p t n", t=4, p=P
+                    ),
                 )
             else:
                 nc.sync.dma_start(out=wrow[0:1, :], in_=kv_norm_w.rearrange("(o n) -> o n", o=1))
@@ -191,13 +195,6 @@ def tile_multiheadlatentattention_pa_kernel(tc, x, Wkv_a, kv_norm_w, Wkv_b, out_
                 live[("xt", a, b)][:].rearrange("p g u r -> p g r u"),
             )
 
-        def x_quantise(a, b):
-            nc.vector.quantize_mx(
-                out=x_codes[a][:, 256 * b : 256 * (b + 1)].bitcast(FP8X4),
-                scales=x_scales[a][:, 256 * b : 256 * (b + 1)],
-                in_=live[("gx", a)][:, 2 * b : 2 * b + 2, :, :].rearrange("p g r u -> p (g r u)").bitcast(BF16),
-            )
-
         def first_matmul(a, dst, c0, c1):
             for g in range(4):
                 nc.tensor.matmul_mx(
@@ -211,10 +208,14 @@ def tile_multiheadlatentattention_pa_kernel(tc, x, Wkv_a, kv_norm_w, Wkv_b, out_
                 )
 
         def wb_regroup(j):
-            cc, kv = j // 2, j % 2
-            t = stage.tile([P, 512, 4], BF16, name="gb", tag="gb", align_bytes=64)
+            cc, kv = PIECE[j]
+            t = stage.tile([P, 512, 4], BF16, name="gb", tag="gb", bufs=3, align_bytes=64)
             live[("gb", j)] = t
-            src = wb_raw[cc][:].rearrange("p t (h k c i) -> p t h k c i", h=4, k=2, c=32, i=4)
+            load = (0, 1, 1, 2)[cc]
+            first = 1024 * (cc - WB_LOAD[load][0])
+            src = wb_raw[load][:, :, first : first + 1024].rearrange(
+                "p t (h k c i) -> p t h k c i", h=4, k=2, c=32, i=4
+            )
             nc.vector.tensor_copy(
                 out=t[:].rearrange("p (h c i) t -> p h c t i", h=4, c=32, i=4),
                 in_=src[:, :, :, kv, :, :].rearrange("p t h c i -> p h c t i"),
@@ -235,7 +236,7 @@ def tile_multiheadlatentattention_pa_kernel(tc, x, Wkv_a, kv_norm_w, Wkv_b, out_
             elif kind == "Wm":
                 nc.scalar.activation(out=warm[:, 1:2], in_=eps_t[:], func=ACT.Sqrt)
             elif kind == "Gc":
-                nc.vector.tensor_copy(out=gain[:], in_=live["gain_ps"][:])
+                nc.scalar.copy(out=gain[:], in_=live["gain_ps"][:])
             elif kind == "Rv":
                 wa_regroup(op[1], "V", 0, WA_V_COLS)
             elif kind == "Rs":
@@ -252,17 +253,19 @@ def tile_multiheadlatentattention_pa_kernel(tc, x, Wkv_a, kv_norm_w, Wkv_b, out_
                 x_copy(op[1], 0, op[2])
             elif kind == "cB":
                 x_copy(op[1], 1, op[2])
-            elif kind == "QA":
-                x_quantise(op[1], 0)
-            elif kind == "QB":
-                x_quantise(op[1], 1)
+            elif kind == "Q":
+                nc.vector.quantize_mx(
+                    out=x_codes[op[1]][:].bitcast(FP8X4),
+                    scales=x_scales[op[1]][:],
+                    in_=live[("gx", op[1])][:].rearrange("p g r u -> p (g r u)").bitcast(BF16),
+                )
             elif kind == "M":
                 live[("c", op[1])] = psum.tile([P, LORA], F32, name="c_ps", tag="ps")
                 first_matmul(op[1], live[("c", op[1])][:], 0, LORA)
             elif kind == "RP":
                 first_matmul(op[1], rope_ps[:, op[1], :], LORA, A_COLS)
             elif kind == "SQ":
-                junk = stage.tile([P, LORA], BF16, name="junk", tag="junk")
+                junk = stage.tile([P, LORA], BF16, name="junk", tag="junk", bufs=2)
                 nc.scalar.activation(out=junk[:], in_=live[("c", op[1])][:], func=ACT.Square, accum_out=sumsq[op[1]][:])
             elif kind == "RT":
                 nc.scalar.activation(
@@ -312,11 +315,18 @@ def tile_multiheadlatentattention_pa_kernel(tc, x, Wkv_a, kv_norm_w, Wkv_b, out_
                 )
             elif kind == "d":
                 a, j = op[1], op[2]
-                st = outp.tile([P, 512], F32, name="st", tag="st")
-                copy_on(op[3], st[:], live[("o", a, j)][:])
-                nc.sync.dma_start(
-                    out=outs[j % 2][P * a : P * (a + 1), 512 * (j // 2) : 512 * (j // 2 + 1)], in_=st[:]
-                )
+                cc, kv = PIECE[j]
+                rows = outs[kv][P * a : P * (a + 1), :]
+                if cc == 0 or cc == 3:
+                    st = outp.tile([P, 512], F32, name="st", tag="st")
+                    copy_on(op[3], st[:], live[("o", a, j)][:])
+                    nc.sync.dma_start(out=rows[:, 512 * cc : 512 * (cc + 1)], in_=st[:])
+                elif cc == 1:
+                    live[("st2", a, kv)] = outp.tile([P, 1024], F32, name="st2", tag="st2", bufs=5)
+                    copy_on(op[3], live[("st2", a, kv)][:, 0:512], live[("o", a, j)][:])
+                else:
+                    copy_on(op[3], live[("st2", a, kv)][:, 512:1024], live[("o", a, j)][:])
+                    nc.sync.dma_start(out=rows[:, 512:1536], in_=live[("st2", a, kv)][:])
             elif kind == "ro":
                 if op[1] == 1:
                     nc.vector.tensor_tensor(

@@ -13,344 +13,384 @@ ALU = mybir.AluOpType
 ACT = mybir.ActivationFunctionType
 
 P = 128
-TOK = 512
+PACK = 4
+K_PASS = P * PACK
+TOKENS = 512
+TILES = TOKENS // P
+SEQ_HALVES = 2
 D_MODEL = 2048
-LORA = 512
+PASSES = D_MODEL // K_PASS
+LATENT = 512
 ROPE = 128
-A_COLS = LORA + ROPE
+ROPE_PAIRS = ROPE // 2
+A_COLS = LATENT + ROPE
 KV_COLS = 4096
+HEAD_DIM = 128
+CHUNK_COLS = 1024
+CHUNK_HEADS = CHUNK_COLS // (2 * HEAD_DIM)
+CHUNKS = KV_COLS // CHUNK_COLS
+PIECE_COLS = CHUNK_HEADS * HEAD_DIM
+PIECES = 2 * CHUNKS
 RMS_EPS = 1.1920928955078125e-07
 ROPE_BASE = 10000.0
 TWO_PI = 6.283185307179586
 
-FLOPS = 2 * TOK * D_MODEL * A_COLS + 2 * TOK * LORA * KV_COLS
+FLOPS = 2 * TOKENS * D_MODEL * A_COLS + 2 * TOKENS * LATENT * KV_COLS
 
-WB_LOAD = ((0, 1), (1, 2), (3, 1))
-PIECE = ((0, 0), (0, 1), (1, 0), (2, 0), (1, 1), (2, 1), (3, 0), (3, 1))
-WA_V_COLS = 320
-LOADS = (("Wa", 0), ("Wa", 1), ("Wa", 2), ("Wa", 3), ("w", 0), ("x", 0), ("x", 1), ("Wb", 0), ("x", 2), ("x", 3), ("Wb", 1), ("Wb", 2))
-
-PLAN = (
-    ("Rs", 0), ("Rv", 0), ("Sin",), ("Rv", 1), ("Rs", 1), ("Qc", 0),
-    ("Qr", 0), ("Rv", 2), ("Rs", 2), ("Qc", 1), ("G",), ("Rv", 3),
-    ("Rs", 3), ("Gc",), ("TA", 0), ("TB", 0), ("Qc", 2), ("cA", 0, "S"),
-    ("Qc", 3), ("TA", 1), ("cB", 0, "S"), ("TB", 1), ("cA", 1, "S"), ("Q", 0),
-    ("cB", 1, "S"), ("Qr", 1), ("M", 0), ("Wm",), ("Qr", 2), ("Q", 1),
-    ("Qr", 3), ("WR", 0), ("M", 1), ("SQ", 0), ("WQ", 0), ("RT", 0),
-    ("TA", 2), ("SQ", 1), ("WR", 1), ("TB", 2), ("TA", 3), ("RT", 1),
-    ("TB", 3), ("cA", 2, "S"), ("RP", 0), ("RC", 0), ("cB", 2, "S"), ("NM", 0),
-    ("RP", 1), ("cA", 3, "S"), ("RC", 1), ("NM", 1), ("N", 0), ("cB", 3, "S"),
-    ("N", 1), ("cN", 0, "S"), ("Q", 2), ("cN", 1, "S"), ("QN", 0), ("M", 2),
-    ("Q", 3), ("QN", 1), ("WQ", 1), ("P", 0, 0), ("WR", 2), ("SQ", 2),
-    ("P", 1, 0), ("P", 0, 1), ("M", 3), ("d", 0, 0, "S"), ("WQ", 2), ("d", 1, 0, "S"),
-    ("WR", 3), ("P", 1, 1), ("RT", 2), ("d", 0, 1, "S"), ("RP", 2), ("P", 0, 2),
-    ("SQ", 3), ("P", 1, 2), ("RP", 3), ("RC", 2), ("NM", 2), ("RT", 3),
-    ("d", 1, 1, "S"), ("RC", 3), ("NM", 3), ("N", 2), ("d", 0, 2, "S"), ("WQ", 3),
-    ("cN", 2, "S"), ("N", 3), ("cN", 3, "S"), ("WR", 4), ("P", 0, 3), ("d", 1, 2, "S"),
-    ("P", 1, 3), ("d", 0, 3, "S"), ("QN", 2), ("QN", 3), ("WQ", 4), ("d", 1, 3, "S"),
-    ("P", 2, 0), ("P", 3, 0), ("WR", 5), ("d", 2, 0, "S"), ("P", 2, 1), ("P", 3, 1),
-    ("d", 3, 0, "S"), ("P", 2, 2), ("P", 3, 2), ("d", 2, 1, "S"), ("P", 2, 3), ("WQ", 5),
-    ("ro", 1), ("ro", 2), ("ro", 3), ("ro", 4), ("P", 3, 3), ("d", 3, 1, "S"),
-    ("P", 0, 4), ("WR", 6), ("P", 1, 4), ("d", 2, 2, "S"), ("P", 2, 4), ("P", 3, 4),
-    ("d", 3, 2, "S"), ("WQ", 6), ("P", 0, 5), ("d", 2, 3, "S"), ("d", 3, 4, "V"), ("P", 1, 5),
-    ("d", 3, 3, "S"), ("P", 2, 5), ("WR", 7), ("d", 0, 4, "S"), ("P", 3, 5), ("P", 0, 6),
-    ("d", 1, 4, "S"), ("P", 1, 6), ("d", 2, 4, "S"), ("d", 3, 5, "V"), ("P", 2, 6), ("d", 0, 5, "S"),
-    ("WQ", 7), ("P", 3, 6), ("d", 1, 5, "S"), ("d", 3, 6, "V"), ("d", 2, 5, "S"), ("P", 0, 7),
-    ("P", 1, 7), ("d", 0, 6, "S"), ("P", 2, 7), ("P", 3, 7), ("d", 1, 7, "V"), ("d", 1, 6, "S"),
-    ("d", 2, 6, "S"), ("d", 3, 7, "V"), ("d", 0, 7, "S"), ("d", 2, 7, "S"),
-)
+WA_VECTOR_COLS = 320
+FIRST_PIECE_VECTOR_EMPTIES = 4
+RUN = 4
 
 
 def tile_multiheadlatentattention_pa_kernel(tc, x, Wkv_a, kv_norm_w, Wkv_b, out_0, out_1, out_2):
     nc = tc.nc
-    xf = x.flatten_outer_dims()
-    outs = [
+    x_rows = x.flatten_outer_dims()
+    kv_out = [
         out_0.rearrange("b s h d -> (b s) (h d)"),
         out_1.rearrange("b s h d -> (b s) (h d)"),
     ]
     with ExitStack() as ctx:
         keep = ctx.enter_context(tc.tile_pool(name="keep", bufs=1))
-        stage = ctx.enter_context(tc.tile_pool(name="stage", bufs=4))
-        outp = ctx.enter_context(tc.tile_pool(name="outp", bufs=8))
-        psum = ctx.enter_context(tc.psum_pool(name="psum", bufs=7))
-        psr = ctx.enter_context(tc.psum_pool(name="psr", bufs=1))
+        regrouped = ctx.enter_context(tc.tile_pool(name="regrouped", bufs=3))
+        scrap = ctx.enter_context(tc.tile_pool(name="scrap", bufs=2))
+        leaving = ctx.enter_context(tc.tile_pool(name="leaving", bufs=12))
+        banks = ctx.enter_context(tc.psum_pool(name="banks", bufs=7))
+        rope_bank = ctx.enter_context(tc.psum_pool(name="rope_bank", bufs=1))
         ctx.enter_context(tc.manual_schedule())
 
-        eps_t = keep.tile([P, 1], F32, name="eps_t")
-        nc.vector.memset(eps_t[:], RMS_EPS)
-        warm = keep.tile([P, 2], F32, name="warm")
-        nc.scalar.activation(out=warm[:, 0:1], in_=eps_t[:], func=ACT.Sin)
-        wrow = keep.tile([P, LORA], BF16, name="wrow")
-        nc.vector.memset(wrow[:], 0.0)
-        pos_i = keep.tile([P, 2], I32, name="pos_i")
-        nc.gpsimd.iota(pos_i[:], pattern=[[P, 2]], base=0, channel_multiplier=1)
+        wa_raw = [keep.tile([P, PACK, A_COLS], BF16, name="wa_raw%d" % g) for g in range(PASSES)]
+        wa_grouped = [
+            keep.tile([P, A_COLS, PACK], BF16, name="wa_grouped%d" % g, align_bytes=64) for g in range(PASSES)
+        ]
+        wa_codes = keep.tile([P, PASSES, A_COLS], U32, name="wa_codes", align_bytes=64)
+        wa_scales = keep.tile([P, PASSES, A_COLS], U8, name="wa_scales", align_bytes=64)
+        x_raw = [keep.tile([P, D_MODEL], BF16, name="x_raw%d" % a) for a in range(TILES)]
+        x_grouped = [keep.tile([P, PASSES, P, 2], F32, name="x_grouped%d" % a, align_bytes=64) for a in range(TILES)]
+        x_codes = [keep.tile([P, PASSES * P], U32, name="x_codes%d" % a, align_bytes=64) for a in range(TILES)]
+        x_scales = [keep.tile([P, PASSES * P], U8, name="x_scales%d" % a, align_bytes=64) for a in range(TILES)]
+        sum_squares = [keep.tile([P, 1], F32, name="sum_squares%d" % a) for a in range(TILES)]
+        rms = [keep.tile([P, 1], F32, name="rms%d" % a) for a in range(TILES)]
+        inv_rms = [keep.tile([P, 1], F32, name="inv_rms%d" % a) for a in range(TILES)]
+        normed = [keep.tile([P, LATENT], BF16, name="normed%d" % a) for a in range(TILES)]
+        n_grouped = [keep.tile([P, P, PACK], BF16, name="n_grouped%d" % a, align_bytes=64) for a in range(TILES)]
+        n_codes = [keep.tile([P, P], U32, name="n_codes%d" % a, align_bytes=64) for a in range(TILES)]
+        n_scales = [keep.tile([P, P], U8, name="n_scales%d" % a, align_bytes=64) for a in range(TILES)]
+        wb_raw = [keep.tile([P, PACK, CHUNK_COLS], BF16, name="wb_raw%d" % c) for c in range(CHUNKS)]
+        wb_codes = keep.tile([P, PIECES, PIECE_COLS], U32, name="wb_codes", align_bytes=64)
+        wb_scales = keep.tile([P, PIECES, PIECE_COLS], U8, name="wb_scales", align_bytes=64)
+        raw_rope = rope_bank.tile([P, TILES, ROPE], F32, name="raw_rope")
+        in_psum = {}
+        wb_grouped = {}
 
-        wa_raw = [keep.tile([P, 4, A_COLS], BF16, name="wa_raw%d" % g) for g in range(4)]
-        x_raw = [keep.tile([P, D_MODEL], BF16, name="x_raw%d" % a) for a in range(4)]
-        wb_raw = [keep.tile([P, 4, 1024 * WB_LOAD[c][1]], BF16, name="wb_raw%d" % c) for c in range(3)]
-        for what, i in LOADS:
-            if what == "Wa":
-                nc.sync.dma_start(
-                    out=wa_raw[i][:].rearrange("p (u e) c -> p u (e c)", u=2, e=2),
-                    in_=Wkv_a[512 * i : 512 * (i + 1), :].rearrange("(u p e) c -> p u (e c)", u=2, p=P, e=2),
-                )
-            elif what == "x":
-                nc.sync.dma_start(out=x_raw[i][:], in_=xf[P * i : P * (i + 1), :])
-            elif what == "Wb":
-                nc.sync.dma_start(
-                    out=wb_raw[i][:],
-                    in_=Wkv_b[:, 1024 * WB_LOAD[i][0] : 1024 * (WB_LOAD[i][0] + WB_LOAD[i][1])].rearrange(
-                        "(t p) n -> p t n", t=4, p=P
-                    ),
-                )
-            else:
-                nc.sync.dma_start(out=wrow[0:1, :], in_=kv_norm_w.rearrange("(o n) -> o n", o=1))
+        eps = keep.tile([P, 1], F32, name="eps")
+        nc.vector.memset(eps[:], RMS_EPS)
+        table_loaded = keep.tile([P, 2], F32, name="table_loaded")
+        nc.scalar.activation(out=table_loaded[:, 0:1], in_=eps[:], func=ACT.Sin)
+        gain_row = keep.tile([P, LATENT], BF16, name="gain_row")
+        nc.vector.memset(gain_row[:], 0.0)
+        position_int = keep.tile([P, SEQ_HALVES], I32, name="position_int")
+        nc.gpsimd.iota(position_int[:], pattern=[[P, SEQ_HALVES]], base=0, channel_multiplier=1)
 
-        freq = keep.tile([P, 64], F32, name="freq")
-        nc.vector.memset(freq[:, 0:1], 1.0)
-        for j in range(6):
-            w = 2 ** j
-            nc.vector.tensor_scalar_mul(
-                out=freq[:, w : 2 * w], in0=freq[:, 0:w], scalar1=ROPE_BASE ** (-2.0 * w / ROPE)
+        def load_wa(g):
+            nc.sync.dma_start(
+                out=wa_raw[g][:].rearrange("p (u e) c -> p u (e c)", u=2, e=2),
+                in_=Wkv_a[K_PASS * g : K_PASS * (g + 1), :].rearrange("(u p e) c -> p u (e c)", u=2, p=P, e=2),
             )
-        pos_f = keep.tile([P, 2], F32, name="pos_f")
-        nc.vector.tensor_copy(out=pos_f[:], in_=pos_i[:])
-        turns = keep.tile([P, 2, 2, 64], F32, name="turns")
-        for h in range(2):
+
+        def load_x(a):
+            nc.sync.dma_start(out=x_raw[a][:], in_=x_rows[P * a : P * (a + 1), :])
+
+        def load_wb(c):
+            nc.sync.dma_start(
+                out=wb_raw[c][:],
+                in_=Wkv_b[:, CHUNK_COLS * c : CHUNK_COLS * (c + 1)].rearrange("(t p) n -> p t n", t=PACK, p=P),
+            )
+
+        for g in range(PASSES):
+            load_wa(g)
+        nc.sync.dma_start(out=gain_row[0:1, :], in_=kv_norm_w.rearrange("(o n) -> o n", o=1))
+        load_x(0)
+        load_x(1)
+        load_wb(0)
+        load_x(2)
+        load_x(3)
+        for c in range(1, CHUNKS):
+            load_wb(c)
+
+        frequency = keep.tile([P, ROPE_PAIRS], F32, name="frequency")
+        nc.vector.memset(frequency[:, 0:1], 1.0)
+        for filled in (1, 2, 4, 8, 16, 32):
+            nc.vector.tensor_scalar_mul(
+                out=frequency[:, filled : 2 * filled],
+                in0=frequency[:, 0:filled],
+                scalar1=ROPE_BASE ** (-2.0 * filled / ROPE),
+            )
+        position = keep.tile([P, SEQ_HALVES], F32, name="position")
+        nc.vector.tensor_copy(out=position[:], in_=position_int[:])
+        turns = keep.tile([P, 2, SEQ_HALVES, ROPE_PAIRS], F32, name="turns")
+        for half in range(SEQ_HALVES):
             nc.vector.tensor_scalar(
-                out=turns[:, 0, h, :], in0=freq[:], scalar1=pos_f[:, h : h + 1], scalar2=1.0 / TWO_PI,
-                op0=ALU.mult, op1=ALU.mult,
+                out=turns[:, 0, half, :],
+                in0=frequency[:],
+                scalar1=position[:, half : half + 1],
+                scalar2=1.0 / TWO_PI,
+                op0=ALU.mult,
+                op1=ALU.mult,
             )
         nc.vector.tensor_scalar_add(out=turns[:, 1, :, :], in0=turns[:, 0, :, :], scalar1=0.25)
-        turns_flat = turns[:].rearrange("p s h i -> p (s h i)")
-        whole_i = keep.tile([P, 256], I32, name="whole_i")
-        nc.vector.tensor_copy(out=whole_i[:], in_=turns_flat)
-        whole_f = keep.tile([P, 256], F32, name="whole_f")
-        nc.vector.tensor_copy(out=whole_f[:], in_=whole_i[:])
-        frac = keep.tile([P, 256], F32, name="frac")
-        nc.vector.tensor_tensor(out=frac[:], in0=turns_flat, in1=whole_f[:], op=ALU.subtract)
-        trig = keep.tile([P, 3, P], F32, name="trig")
+        turns_row = turns[:].rearrange("p s h i -> p (s h i)")
+        whole_int = keep.tile([P, 2 * P], I32, name="whole_int")
+        nc.vector.tensor_copy(out=whole_int[:], in_=turns_row)
+        whole = keep.tile([P, 2 * P], F32, name="whole")
+        nc.vector.tensor_copy(out=whole[:], in_=whole_int[:])
+        part_turn = keep.tile([P, 2 * P], F32, name="part_turn")
+        nc.vector.tensor_tensor(out=part_turn[:], in0=turns_row, in1=whole[:], op=ALU.subtract)
+        SIN, COS, MINUS_SIN = 0, 1, 2
+        trig = keep.tile([P, 3, SEQ_HALVES * ROPE_PAIRS], F32, name="trig")
+
         ones = keep.tile([P, P], BF16, name="ones")
         nc.vector.memset(ones[:], 1.0)
-        ident_f = keep.tile([P, P], F32, name="ident_f")
-        make_identity(nc, ident_f[:])
-        ident_b = keep.tile([P, P], BF16, name="ident_b")
-        make_identity(nc, ident_b[:])
+        identity_f32 = keep.tile([P, P], F32, name="identity_f32")
+        make_identity(nc, identity_f32[:])
+        identity_bf16 = keep.tile([P, P], BF16, name="identity_bf16")
+        make_identity(nc, identity_bf16[:])
+        gain = keep.tile([P, LATENT], F32, name="gain")
 
-        gain = keep.tile([P, LORA], F32, name="gain")
-        wa_codes = keep.tile([P, 4, A_COLS], U32, name="wa_codes", align_bytes=64)
-        wa_scales = keep.tile([P, 4, A_COLS], U8, name="wa_scales", align_bytes=64)
-        x_codes = [keep.tile([P, 512], U32, name="x_codes%d" % a, align_bytes=64) for a in range(4)]
-        x_scales = [keep.tile([P, 512], U8, name="x_scales%d" % a, align_bytes=64) for a in range(4)]
-        n_codes = [keep.tile([P, P], U32, name="n_codes%d" % a, align_bytes=64) for a in range(4)]
-        n_scales = [keep.tile([P, P], U8, name="n_scales%d" % a, align_bytes=64) for a in range(4)]
-        sumsq = [keep.tile([P, 1], F32, name="sumsq%d" % a) for a in range(4)]
-        rms = [keep.tile([P, 1], F32, name="rms%d" % a) for a in range(4)]
-        rstd = [keep.tile([P, 1], F32, name="rstd%d" % a) for a in range(4)]
-        wb_codes = keep.tile([P, 8, 512], U32, name="wb_codes", align_bytes=64)
-        wb_scales = keep.tile([P, 8, 512], U8, name="wb_scales", align_bytes=64)
-        rope_ps = psr.tile([P, 4, ROPE], F32, name="rope_ps")
-        straight = keep.tile([P, 2, P, 2], F32, name="straight")
-        crossed = keep.tile([P, 2, 2, P], F32, name="crossed")
-        turned = keep.tile([P, 2, P, 2], F32, name="turned")
-        live = {}
-
-        def copy_on(engine, out, in_):
-            if engine == "V":
-                nc.vector.tensor_copy(out=out, in_=in_)
-            else:
-                nc.scalar.copy(out=out, in_=in_)
-
-        def wa_regroup(g, engine, c0, c1):
-            if ("ga", g) not in live:
-                live[("ga", g)] = stage.tile([P, A_COLS, 4], BF16, name="ga", tag="ga", align_bytes=64)
-            copy_on(
-                engine,
-                live[("ga", g)][:, c0:c1, :].rearrange("p (c i) t -> p c t i", i=4),
-                wa_raw[g][:, :, c0:c1].rearrange("p t (c i) -> p c t i", i=4),
+        def rope_tables_scalar():
+            nc.scalar.activation(
+                out=trig[:, SIN : COS + 1, :].rearrange("p s n -> p (s n)"), in_=part_turn[:], func=ACT.Sin, scale=TWO_PI
             )
+            nc.scalar.activation(out=trig[:, MINUS_SIN, :], in_=part_turn[:, 0:P], func=ACT.Sin, scale=-TWO_PI)
 
-        def wa_quantise(g, c0, c1):
+        def load_sqrt_table():
+            nc.scalar.activation(out=table_loaded[:, 1:2], in_=eps[:], func=ACT.Sqrt)
+
+        def regroup_wa(g):
+            for copy, first, last in (
+                (nc.scalar.copy, WA_VECTOR_COLS, A_COLS),
+                (nc.vector.tensor_copy, 0, WA_VECTOR_COLS),
+            ):
+                copy(
+                    out=wa_grouped[g][:, first:last, :].rearrange("p (c i) t -> p c t i", i=RUN),
+                    in_=wa_raw[g][:, :, first:last].rearrange("p t (c i) -> p c t i", i=RUN),
+                )
+
+        def quantise_wa(g, first, last):
             nc.vector.quantize_mx(
-                out=wa_codes[:, g, c0:c1].bitcast(FP8X4),
-                scales=wa_scales[:, g, c0:c1],
-                in_=live[("ga", g)][:, c0:c1, :].rearrange("p c t -> p (c t)"),
+                out=wa_codes[:, g, first:last].bitcast(FP8X4),
+                scales=wa_scales[:, g, first:last],
+                in_=wa_grouped[g][:, first:last, :].rearrange("p c t -> p (c t)"),
             )
 
-        def x_transpose(a, b):
+        def spread_gain():
+            summed = banks.tile([P, LATENT], F32, name="summed", tag="bank")
+            nc.tensor.matmul(out=summed[:], lhsT=ones[:], rhs=gain_row[:], start=True, stop=True)
+            nc.vector.tensor_copy(out=gain[:], in_=summed[:])
+
+        def transpose_x(a):
             words = x_raw[a][:].bitcast(F32)
-            xt = psum.tile([P, 2, 2, P], F32, name="xt", tag="ps")
-            live[("xt", a, b)] = xt
-            for gg in range(2):
-                for u in range(2):
-                    w0 = 256 * (2 * b + gg) + P * u
-                    nc.tensor.transpose(xt[:, gg, u, :], words[:, w0 : w0 + P], ident_f[:])
+            for first_pass in range(0, PASSES, 2):
+                turned = banks.tile([P, 2, 2, P], F32, name="turned", tag="bank")
+                for g in range(2):
+                    for u in range(2):
+                        first_word = 2 * P * (first_pass + g) + P * u
+                        nc.tensor.transpose(turned[:, g, u, :], words[:, first_word : first_word + P], identity_f32[:])
+                nc.scalar.copy(
+                    out=x_grouped[a][:, first_pass : first_pass + 2, :, :],
+                    in_=turned[:].rearrange("p g u r -> p g r u"),
+                )
 
-        def x_copy(a, b, engine):
-            if ("gx", a) not in live:
-                live[("gx", a)] = stage.tile([P, 4, P, 2], F32, name="gx", tag="gx", align_bytes=64)
-            copy_on(
-                engine,
-                live[("gx", a)][:, 2 * b : 2 * b + 2, :, :],
-                live[("xt", a, b)][:].rearrange("p g u r -> p g r u"),
+        def quantise_x(a):
+            nc.vector.quantize_mx(
+                out=x_codes[a][:].bitcast(FP8X4),
+                scales=x_scales[a][:],
+                in_=x_grouped[a][:].rearrange("p g r u -> p (g r u)").bitcast(BF16),
             )
 
-        def first_matmul(a, dst, c0, c1):
-            for g in range(4):
+        def first_matmul(a, out, first, last):
+            for g in range(PASSES):
                 nc.tensor.matmul_mx(
-                    out=dst,
+                    out=out,
                     lhsT=x_codes[a][:, P * g : P * (g + 1)].bitcast(FP8X4),
                     lhsT_scale=x_scales[a][:, P * g : P * (g + 1)],
-                    rhs=wa_codes[:, g, c0:c1].bitcast(FP8X4),
-                    rhs_scale=wa_scales[:, g, c0:c1],
+                    rhs=wa_codes[:, g, first:last].bitcast(FP8X4),
+                    rhs_scale=wa_scales[:, g, first:last],
                     start=(g == 0),
-                    stop=(g == 3),
+                    stop=(g == PASSES - 1),
                 )
 
-        def wb_regroup(j):
-            cc, kv = PIECE[j]
-            t = stage.tile([P, 512, 4], BF16, name="gb", tag="gb", bufs=3, align_bytes=64)
-            live[("gb", j)] = t
-            load = (0, 1, 1, 2)[cc]
-            first = 1024 * (cc - WB_LOAD[load][0])
-            src = wb_raw[load][:, :, first : first + 1024].rearrange(
-                "p t (h k c i) -> p t h k c i", h=4, k=2, c=32, i=4
+        def latent(a):
+            in_psum["latent", a] = banks.tile([P, LATENT], F32, name="latent", tag="bank")
+            first_matmul(a, in_psum["latent", a][:], 0, LATENT)
+            squares = scrap.tile([P, LATENT], BF16, name="squares")
+            nc.scalar.activation(out=squares[:], in_=in_psum["latent", a][:], func=ACT.Square, accum_out=sum_squares[a][:])
+            nc.scalar.activation(out=rms[a][:], in_=sum_squares[a][:], func=ACT.Sqrt, scale=1.0 / LATENT, bias=eps[:])
+
+        def rope_key(a):
+            first_matmul(a, raw_rope[:, a, :], LATENT, A_COLS)
+
+        def normalise(a):
+            nc.vector.reciprocal(out=inv_rms[a][:], in_=rms[a][:])
+            nc.vector.scalar_tensor_tensor(
+                out=normed[a][:],
+                in0=in_psum["latent", a][:],
+                scalar=inv_rms[a][:],
+                in1=gain[:],
+                op0=ALU.mult,
+                op1=ALU.mult,
+            )
+
+        def transpose_n(a):
+            turned = banks.tile([P, PACK, P], BF16, name="turned_n", tag="bank")
+            for t in range(PACK):
+                nc.tensor.transpose(turned[:, t, :], normed[a][:, P * t : P * (t + 1)], identity_bf16[:])
+            nc.scalar.copy(out=n_grouped[a][:], in_=turned[:].rearrange("p t r -> p r t"))
+
+        def quantise_n(a):
+            nc.vector.quantize_mx(
+                out=n_codes[a][:].bitcast(FP8X4),
+                scales=n_scales[a][:],
+                in_=n_grouped[a][:].rearrange("p r t -> p (r t)"),
+            )
+
+        def regroup_wb(j):
+            wb_grouped[j] = regrouped.tile([P, PIECE_COLS, PACK], BF16, name="wb_grouped", align_bytes=64)
+            by_head = wb_raw[j // 2][:].rearrange(
+                "p t (h k c i) -> p t h k c i", h=CHUNK_HEADS, k=2, c=HEAD_DIM // RUN, i=RUN
             )
             nc.vector.tensor_copy(
-                out=t[:].rearrange("p (h c i) t -> p h c t i", h=4, c=32, i=4),
-                in_=src[:, :, :, kv, :, :].rearrange("p t h c i -> p h c t i"),
+                out=wb_grouped[j][:].rearrange("p (h c i) t -> p h c t i", h=CHUNK_HEADS, c=HEAD_DIM // RUN, i=RUN),
+                in_=by_head[:, :, :, j % 2, :, :].rearrange("p t h c i -> p h c t i"),
             )
 
-        r4 = rope_ps[:].rearrange("p (b h) (i e) -> p b (h i) e", b=2, e=2)
+        def quantise_wb(j):
+            nc.vector.quantize_mx(
+                out=wb_codes[:, j, :].bitcast(FP8X4),
+                scales=wb_scales[:, j, :],
+                in_=wb_grouped[j][:].rearrange("p c t -> p (c t)"),
+            )
 
-        def emit(op):
-            kind = op[0]
-            if kind == "G":
-                live["gain_ps"] = psum.tile([P, LORA], F32, name="gain_ps", tag="ps")
-                nc.tensor.matmul(out=live["gain_ps"][:], lhsT=ones[:], rhs=wrow[:], start=True, stop=True)
-            elif kind == "Sin":
-                nc.scalar.activation(
-                    out=trig[:, 0:2, :].rearrange("p s n -> p (s n)"), in_=frac[:], func=ACT.Sin, scale=TWO_PI
-                )
-                nc.scalar.activation(out=trig[:, 2, :], in_=frac[:, 0:P], func=ACT.Sin, scale=-TWO_PI)
-            elif kind == "Wm":
-                nc.scalar.activation(out=warm[:, 1:2], in_=eps_t[:], func=ACT.Sqrt)
-            elif kind == "Gc":
-                nc.scalar.copy(out=gain[:], in_=live["gain_ps"][:])
-            elif kind == "Rv":
-                wa_regroup(op[1], "V", 0, WA_V_COLS)
-            elif kind == "Rs":
-                wa_regroup(op[1], "S", WA_V_COLS, A_COLS)
-            elif kind == "Qc":
-                wa_quantise(op[1], 0, LORA)
-            elif kind == "Qr":
-                wa_quantise(op[1], LORA, A_COLS)
-            elif kind == "TA":
-                x_transpose(op[1], 0)
-            elif kind == "TB":
-                x_transpose(op[1], 1)
-            elif kind == "cA":
-                x_copy(op[1], 0, op[2])
-            elif kind == "cB":
-                x_copy(op[1], 1, op[2])
-            elif kind == "Q":
-                nc.vector.quantize_mx(
-                    out=x_codes[op[1]][:].bitcast(FP8X4),
-                    scales=x_scales[op[1]][:],
-                    in_=live[("gx", op[1])][:].rearrange("p g r u -> p (g r u)").bitcast(BF16),
-                )
-            elif kind == "M":
-                live[("c", op[1])] = psum.tile([P, LORA], F32, name="c_ps", tag="ps")
-                first_matmul(op[1], live[("c", op[1])][:], 0, LORA)
-            elif kind == "RP":
-                first_matmul(op[1], rope_ps[:, op[1], :], LORA, A_COLS)
-            elif kind == "SQ":
-                junk = stage.tile([P, LORA], BF16, name="junk", tag="junk", bufs=2)
-                nc.scalar.activation(out=junk[:], in_=live[("c", op[1])][:], func=ACT.Square, accum_out=sumsq[op[1]][:])
-            elif kind == "RT":
-                nc.scalar.activation(
-                    out=rms[op[1]][:], in_=sumsq[op[1]][:], func=ACT.Sqrt, scale=1.0 / LORA, bias=eps_t[:]
-                )
-            elif kind == "RC":
-                nc.vector.reciprocal(out=rstd[op[1]][:], in_=rms[op[1]][:])
-            elif kind == "NM":
-                live[("n", op[1])] = stage.tile([P, LORA], BF16, name="n_bf", tag="n_bf")
-                nc.vector.scalar_tensor_tensor(
-                    out=live[("n", op[1])][:], in0=live[("c", op[1])][:], scalar=rstd[op[1]][:], in1=gain[:],
-                    op0=ALU.mult, op1=ALU.mult,
-                )
-            elif kind == "N":
-                nt = psum.tile([P, 4, P], BF16, name="nt", tag="ps")
-                live[("nt", op[1])] = nt
-                for t in range(4):
-                    nc.tensor.transpose(nt[:, t, :], live[("n", op[1])][:, P * t : P * (t + 1)], ident_b[:])
-            elif kind == "cN":
-                live[("gn", op[1])] = stage.tile([P, P, 4], BF16, name="gn", tag="gn", align_bytes=64)
-                copy_on(op[2], live[("gn", op[1])][:], live[("nt", op[1])][:].rearrange("p t r -> p r t"))
-            elif kind == "QN":
-                nc.vector.quantize_mx(
-                    out=n_codes[op[1]][:].bitcast(FP8X4),
-                    scales=n_scales[op[1]][:],
-                    in_=live[("gn", op[1])][:].rearrange("p r t -> p (r t)"),
-                )
-            elif kind == "WR":
-                wb_regroup(op[1])
-            elif kind == "WQ":
-                nc.vector.quantize_mx(
-                    out=wb_codes[:, op[1], :].bitcast(FP8X4),
-                    scales=wb_scales[:, op[1], :],
-                    in_=live[("gb", op[1])][:].rearrange("p c t -> p (c t)"),
-                )
-            elif kind == "P":
-                a, j = op[1], op[2]
-                live[("o", a, j)] = psum.tile([P, 512], F32, name="o_ps", tag="ps")
-                nc.tensor.matmul_mx(
-                    out=live[("o", a, j)][:],
-                    lhsT=n_codes[a][:].bitcast(FP8X4),
-                    lhsT_scale=n_scales[a][:],
-                    rhs=wb_codes[:, j, :].bitcast(FP8X4),
-                    rhs_scale=wb_scales[:, j, :],
-                    start=True,
-                    stop=True,
-                )
-            elif kind == "d":
-                a, j = op[1], op[2]
-                cc, kv = PIECE[j]
-                rows = outs[kv][P * a : P * (a + 1), :]
-                if cc == 0 or cc == 3:
-                    st = outp.tile([P, 512], F32, name="st", tag="st")
-                    copy_on(op[3], st[:], live[("o", a, j)][:])
-                    nc.sync.dma_start(out=rows[:, 512 * cc : 512 * (cc + 1)], in_=st[:])
-                elif cc == 1:
-                    live[("st2", a, kv)] = outp.tile([P, 1024], F32, name="st2", tag="st2", bufs=5)
-                    copy_on(op[3], live[("st2", a, kv)][:, 0:512], live[("o", a, j)][:])
-                else:
-                    copy_on(op[3], live[("st2", a, kv)][:, 512:1024], live[("o", a, j)][:])
-                    nc.sync.dma_start(out=rows[:, 512:1536], in_=live[("st2", a, kv)][:])
-            elif kind == "ro":
-                if op[1] == 1:
-                    nc.vector.tensor_tensor(
-                        out=straight[:], in0=r4,
-                        in1=trig[:, 1, :].unsqueeze(1).unsqueeze(3).to_broadcast([P, 2, P, 2]), op=ALU.mult,
-                    )
-                elif op[1] == 2:
-                    nc.vector.tensor_tensor(
-                        out=crossed[:, 0, :, :], in0=r4[:, :, :, 1],
-                        in1=trig[:, 2, :].unsqueeze(1).to_broadcast([P, 2, P]), op=ALU.mult,
-                    )
-                elif op[1] == 3:
-                    nc.vector.tensor_tensor(
-                        out=crossed[:, 1, :, :], in0=r4[:, :, :, 0],
-                        in1=trig[:, 0, :].unsqueeze(1).to_broadcast([P, 2, P]), op=ALU.mult,
-                    )
-                else:
-                    nc.vector.tensor_tensor(
-                        out=turned[:], in0=straight[:], in1=crossed[:].rearrange("p e b n -> p b n e"), op=ALU.add
-                    )
-                    nc.sync.dma_start(
-                        out=out_2.rearrange("b (h p) o d -> p (b h) (o d)", h=2, p=P),
-                        in_=turned[:].rearrange("p b (h i) e -> p (b h) (i e)", h=2),
-                    )
+        def second_matmul(a, j):
+            in_psum["kv", a, j] = banks.tile([P, PIECE_COLS], F32, name="kv", tag="bank")
+            nc.tensor.matmul_mx(
+                out=in_psum["kv", a, j][:],
+                lhsT=n_codes[a][:].bitcast(FP8X4),
+                lhsT_scale=n_scales[a][:],
+                rhs=wb_codes[:, j, :].bitcast(FP8X4),
+                rhs_scale=wb_scales[:, j, :],
+                start=True,
+                stop=True,
+            )
 
-        for op in PLAN:
-            emit(op)
+        def store_kv(a, j):
+            out_tile = leaving.tile([P, PIECE_COLS], F32, name="out_tile")
+            if (a == TILES - 1 and j >= FIRST_PIECE_VECTOR_EMPTIES) or (a == 1 and j == PIECES - 1):
+                nc.vector.tensor_copy(out=out_tile[:], in_=in_psum["kv", a, j][:])
+            else:
+                nc.scalar.copy(out=out_tile[:], in_=in_psum["kv", a, j][:])
+            nc.sync.dma_start(
+                out=kv_out[j % 2][P * a : P * (a + 1), PIECE_COLS * (j // 2) : PIECE_COLS * (j // 2 + 1)],
+                in_=out_tile[:],
+            )
+
+        def kv(tiles, j):
+            for a in tiles:
+                second_matmul(a, j)
+            for a in tiles:
+                store_kv(a, j)
+
+        def rope():
+            pairs = raw_rope[:].rearrange("p (b h) (i e) -> p b (h i) e", b=2, e=2)
+            both = [P, 2, P]
+            by_cos = keep.tile([P, 2, P, 2], F32, name="by_cos")
+            nc.vector.tensor_tensor(
+                out=by_cos[:], in0=pairs, in1=trig[:, COS, :].unsqueeze(1).unsqueeze(3).to_broadcast([P, 2, P, 2]), op=ALU.mult
+            )
+            by_sin = keep.tile([P, 2, 2, P], F32, name="by_sin")
+            nc.vector.tensor_tensor(
+                out=by_sin[:, 0, :, :], in0=pairs[:, :, :, 1], in1=trig[:, MINUS_SIN, :].unsqueeze(1).to_broadcast(both), op=ALU.mult
+            )
+            nc.vector.tensor_tensor(
+                out=by_sin[:, 1, :, :], in0=pairs[:, :, :, 0], in1=trig[:, SIN, :].unsqueeze(1).to_broadcast(both), op=ALU.mult
+            )
+            k_rope = keep.tile([P, 2, P, 2], F32, name="k_rope")
+            nc.vector.tensor_tensor(
+                out=k_rope[:], in0=by_cos[:], in1=by_sin[:].rearrange("p e b n -> p b n e"), op=ALU.add
+            )
+            nc.sync.dma_start(
+                out=out_2.rearrange("b (h p) o d -> p (b h) (o d)", h=SEQ_HALVES, p=P),
+                in_=k_rope[:].rearrange("p b (h i) e -> p (b h) (i e)", h=SEQ_HALVES),
+            )
+
+        regroup_wa(0)
+        rope_tables_scalar()
+        for g in range(PASSES):
+            if g + 1 < PASSES:
+                regroup_wa(g + 1)
+            if g == PASSES - 2:
+                spread_gain()
+            quantise_wa(g, 0, LATENT)
+
+        transpose_x(0)
+        transpose_x(1)
+        load_sqrt_table()
+        quantise_x(0)
+        quantise_x(1)
+        for g in range(PASSES):
+            quantise_wa(g, LATENT, A_COLS)
+        latent(0)
+        latent(1)
+        regroup_wb(0)
+        quantise_wb(0)
+        transpose_x(2)
+        transpose_x(3)
+        normalise(0)
+        normalise(1)
+        regroup_wb(1)
+        rope_key(0)
+        rope_key(1)
+        transpose_n(0)
+        transpose_n(1)
+        quantise_x(2)
+        quantise_x(3)
+        quantise_n(0)
+        quantise_n(1)
+        quantise_wb(1)
+        regroup_wb(2)
+        quantise_wb(2)
+        regroup_wb(3)
+
+        latent(2)
+        kv((0, 1), 0)
+        latent(3)
+        kv((0, 1), 1)
+        normalise(2)
+        normalise(3)
+        quantise_wb(3)
+        regroup_wb(4)
+        rope_key(2)
+        rope_key(3)
+        kv((0, 1), 2)
+        transpose_n(2)
+        transpose_n(3)
+        quantise_n(2)
+        quantise_n(3)
+        kv((0, 1), 3)
+        quantise_wb(4)
+        regroup_wb(5)
+        for j in range(4):
+            kv((2, 3), j)
+        quantise_wb(5)
+        regroup_wb(6)
+
+        for j in range(4, PIECES):
+            for a in range(TILES):
+                second_matmul(a, j)
+            if j + 2 < PIECES:
+                quantise_wb(j + 2)
+            if j == PIECES - 1:
+                rope()
+            for a in range(TILES):
+                store_kv(a, j)
+            if j + 3 < PIECES:
+                regroup_wb(j + 3)

@@ -38,7 +38,7 @@ TWO_PI = 6.283185307179586
 FLOPS = 2 * TOKENS * D_MODEL * A_COLS + 2 * TOKENS * LATENT * KV_COLS
 
 WA_VECTOR_COLS = 320
-FIRST_PIECE_VECTOR_EMPTIES = 4
+FIRST_PIECE_VECTOR_EMPTIES = 5
 RUN = 4
 
 
@@ -175,12 +175,13 @@ def tile_multiheadlatentattention_pa_kernel(tc, x, Wkv_a, kv_norm_w, Wkv_b, out_
                     in_=wa_raw[g][:, :, first:last].rearrange("p t (c i) -> p c t i", i=RUN),
                 )
 
-        def quantise_wa(g, first, last):
-            nc.vector.quantize_mx(
-                out=wa_codes[:, g, first:last].bitcast(FP8X4),
-                scales=wa_scales[:, g, first:last],
-                in_=wa_grouped[g][:, first:last, :].rearrange("p c t -> p (c t)"),
-            )
+        def quantise_wa(g):
+            for first, last in ((0, LATENT), (LATENT, A_COLS)):
+                nc.vector.quantize_mx(
+                    out=wa_codes[:, g, first:last].bitcast(FP8X4),
+                    scales=wa_scales[:, g, first:last],
+                    in_=wa_grouped[g][:, first:last, :].rearrange("p c t -> p (c t)"),
+                )
 
         def spread_gain():
             summed = banks.tile([P, LATENT], F32, name="summed", tag="bank")
@@ -201,11 +202,13 @@ def tile_multiheadlatentattention_pa_kernel(tc, x, Wkv_a, kv_norm_w, Wkv_b, out_
                 )
 
         def quantise_x(a):
-            nc.vector.quantize_mx(
-                out=x_codes[a][:].bitcast(FP8X4),
-                scales=x_scales[a][:],
-                in_=x_grouped[a][:].rearrange("p g r u -> p (g r u)").bitcast(BF16),
-            )
+            for first_pass in range(0, PASSES, 2):
+                columns = slice(P * first_pass, P * (first_pass + 2))
+                nc.vector.quantize_mx(
+                    out=x_codes[a][:, columns].bitcast(FP8X4),
+                    scales=x_scales[a][:, columns],
+                    in_=x_grouped[a][:, first_pass : first_pass + 2, :, :].rearrange("p g r u -> p (g r u)").bitcast(BF16),
+                )
 
         def first_matmul(a, out, first, last):
             for g in range(PASSES):
@@ -240,11 +243,11 @@ def tile_multiheadlatentattention_pa_kernel(tc, x, Wkv_a, kv_norm_w, Wkv_b, out_
                 op1=ALU.mult,
             )
 
-        def transpose_n(a):
+        def transpose_n(a, copy):
             turned = banks.tile([P, PACK, P], BF16, name="turned_n", tag="bank")
             for t in range(PACK):
                 nc.tensor.transpose(turned[:, t, :], normed[a][:, P * t : P * (t + 1)], identity_bf16[:])
-            nc.scalar.copy(out=n_grouped[a][:], in_=turned[:].rearrange("p t r -> p r t"))
+            copy(out=n_grouped[a][:], in_=turned[:].rearrange("p t r -> p r t"))
 
         def quantise_n(a):
             nc.vector.quantize_mx(
@@ -299,21 +302,26 @@ def tile_multiheadlatentattention_pa_kernel(tc, x, Wkv_a, kv_norm_w, Wkv_b, out_
             for a in tiles:
                 store_kv(a, j)
 
-        def rope():
-            pairs = raw_rope[:].rearrange("p (b h) (i e) -> p b (h i) e", b=2, e=2)
-            both = [P, 2, P]
-            by_cos = keep.tile([P, 2, P, 2], F32, name="by_cos")
+        pairs = raw_rope[:].rearrange("p (b h) (i e) -> p b (h i) e", b=2, e=2)
+        both = [P, 2, P]
+        by_cos = keep.tile([P, 2, P, 2], F32, name="by_cos")
+        by_sin = keep.tile([P, 2, 2, P], F32, name="by_sin")
+        k_rope = keep.tile([P, 2, P, 2], F32, name="k_rope")
+
+        def rope_by_cos():
             nc.vector.tensor_tensor(
                 out=by_cos[:], in0=pairs, in1=trig[:, COS, :].unsqueeze(1).unsqueeze(3).to_broadcast([P, 2, P, 2]), op=ALU.mult
             )
-            by_sin = keep.tile([P, 2, 2, P], F32, name="by_sin")
+
+        def rope_by_sin():
             nc.vector.tensor_tensor(
                 out=by_sin[:, 0, :, :], in0=pairs[:, :, :, 1], in1=trig[:, MINUS_SIN, :].unsqueeze(1).to_broadcast(both), op=ALU.mult
             )
             nc.vector.tensor_tensor(
                 out=by_sin[:, 1, :, :], in0=pairs[:, :, :, 0], in1=trig[:, SIN, :].unsqueeze(1).to_broadcast(both), op=ALU.mult
             )
-            k_rope = keep.tile([P, 2, P, 2], F32, name="k_rope")
+
+        def rope_sum():
             nc.vector.tensor_tensor(
                 out=k_rope[:], in0=by_cos[:], in1=by_sin[:].rearrange("p e b n -> p b n e"), op=ALU.add
             )
@@ -329,68 +337,68 @@ def tile_multiheadlatentattention_pa_kernel(tc, x, Wkv_a, kv_norm_w, Wkv_b, out_
                 regroup_wa(g + 1)
             if g == PASSES - 2:
                 spread_gain()
-            quantise_wa(g, 0, LATENT)
+            quantise_wa(g)
 
         transpose_x(0)
         transpose_x(1)
         load_sqrt_table()
         quantise_x(0)
         quantise_x(1)
-        for g in range(PASSES):
-            quantise_wa(g, LATENT, A_COLS)
         latent(0)
         latent(1)
         regroup_wb(0)
         quantise_wb(0)
-        transpose_x(2)
-        transpose_x(3)
         normalise(0)
-        normalise(1)
         regroup_wb(1)
+        normalise(1)
+        transpose_x(2)
+        transpose_n(0, nc.scalar.copy)
+        transpose_x(3)
         rope_key(0)
         rope_key(1)
-        transpose_n(0)
-        transpose_n(1)
-        quantise_x(2)
-        quantise_x(3)
         quantise_n(0)
+        quantise_x(2)
+        transpose_n(1, nc.vector.tensor_copy)
         quantise_n(1)
+        quantise_x(3)
         quantise_wb(1)
         regroup_wb(2)
         quantise_wb(2)
-        regroup_wb(3)
 
+        kv((0,), 0)
         latent(2)
-        kv((0, 1), 0)
+        kv((1,), 0)
         latent(3)
         kv((0, 1), 1)
         normalise(2)
-        normalise(3)
-        quantise_wb(3)
-        regroup_wb(4)
         rope_key(2)
         rope_key(3)
-        kv((0, 1), 2)
-        transpose_n(2)
-        transpose_n(3)
+        rope_by_cos()
+        normalise(3)
+        rope_by_sin()
+        second_matmul(0, 2)
+        second_matmul(1, 2)
+        transpose_n(2, nc.scalar.copy)
+        store_kv(0, 2)
+        transpose_n(3, nc.scalar.copy)
+        store_kv(1, 2)
         quantise_n(2)
+        rope_sum()
+        regroup_wb(3)
         quantise_n(3)
-        kv((0, 1), 3)
-        quantise_wb(4)
-        regroup_wb(5)
-        for j in range(4):
-            kv((2, 3), j)
-        quantise_wb(5)
-        regroup_wb(6)
-
-        for j in range(4, PIECES):
-            for a in range(TILES):
+        for a in (2, 3):
+            for j in range(3):
                 second_matmul(a, j)
-            if j + 2 < PIECES:
-                quantise_wb(j + 2)
-            if j == PIECES - 1:
-                rope()
-            for a in range(TILES):
+        for a in (2, 3):
+            for j in range(3):
                 store_kv(a, j)
-            if j + 3 < PIECES:
-                regroup_wb(j + 3)
+
+        quantise_wb(3)
+        for j in range(4, PIECES - 1):
+            regroup_wb(j)
+            quantise_wb(j)
+        regroup_wb(PIECES - 1)
+        for j in range(3, PIECES):
+            if j == PIECES - 2:
+                quantise_wb(PIECES - 1)
+            kv(range(TILES), j)

@@ -38,7 +38,6 @@ TWO_PI = 6.283185307179586
 FLOPS = 2 * TOKENS * D_MODEL * A_COLS + 2 * TOKENS * LATENT * KV_COLS
 
 WA_VECTOR_COLS = 320
-FIRST_PIECE_VECTOR_EMPTIES = 5
 RUN = 4
 
 
@@ -106,15 +105,14 @@ def tile_multiheadlatentattention_pa_kernel(tc, x, Wkv_a, kv_norm_w, Wkv_b, out_
                 in_=Wkv_b[:, CHUNK_COLS * c : CHUNK_COLS * (c + 1)].rearrange("(t p) n -> p t n", t=PACK, p=P),
             )
 
+        load_x(0)
+        load_x(1)
         for g in range(PASSES):
             load_wa(g)
         nc.sync.dma_start(out=gain_row[0:1, :], in_=kv_norm_w.rearrange("(o n) -> o n", o=1))
-        load_x(0)
-        load_x(1)
-        load_wb(0)
         load_x(2)
         load_x(3)
-        for c in range(1, CHUNKS):
+        for c in range(CHUNKS):
             load_wb(c)
 
         frequency = keep.tile([P, ROPE_PAIRS], F32, name="frequency")
@@ -175,20 +173,19 @@ def tile_multiheadlatentattention_pa_kernel(tc, x, Wkv_a, kv_norm_w, Wkv_b, out_
                     in_=wa_raw[g][:, :, first:last].rearrange("p t (c i) -> p c t i", i=RUN),
                 )
 
-        def quantise_wa(g):
-            for first, last in ((0, LATENT), (LATENT, A_COLS)):
-                nc.vector.quantize_mx(
-                    out=wa_codes[:, g, first:last].bitcast(FP8X4),
-                    scales=wa_scales[:, g, first:last],
-                    in_=wa_grouped[g][:, first:last, :].rearrange("p c t -> p (c t)"),
-                )
+        def quantise_wa(g, first, last):
+            nc.vector.quantize_mx(
+                out=wa_codes[:, g, first:last].bitcast(FP8X4),
+                scales=wa_scales[:, g, first:last],
+                in_=wa_grouped[g][:, first:last, :].rearrange("p c t -> p (c t)"),
+            )
 
         def spread_gain():
             summed = banks.tile([P, LATENT], F32, name="summed", tag="bank")
             nc.tensor.matmul(out=summed[:], lhsT=ones[:], rhs=gain_row[:], start=True, stop=True)
             nc.vector.tensor_copy(out=gain[:], in_=summed[:])
 
-        def transpose_x(a):
+        def transpose_x(a, copy):
             words = x_raw[a][:].bitcast(F32)
             for first_pass in range(0, PASSES, 2):
                 turned = banks.tile([P, 2, 2, P], F32, name="turned", tag="bank")
@@ -196,7 +193,7 @@ def tile_multiheadlatentattention_pa_kernel(tc, x, Wkv_a, kv_norm_w, Wkv_b, out_
                     for u in range(2):
                         first_word = 2 * P * (first_pass + g) + P * u
                         nc.tensor.transpose(turned[:, g, u, :], words[:, first_word : first_word + P], identity_f32[:])
-                nc.scalar.copy(
+                copy(
                     out=x_grouped[a][:, first_pass : first_pass + 2, :, :],
                     in_=turned[:].rearrange("p g u r -> p g r u"),
                 )
@@ -287,7 +284,7 @@ def tile_multiheadlatentattention_pa_kernel(tc, x, Wkv_a, kv_norm_w, Wkv_b, out_
 
         def store_kv(a, j):
             out_tile = leaving.tile([P, PIECE_COLS], F32, name="out_tile")
-            if (a == TILES - 1 and j >= FIRST_PIECE_VECTOR_EMPTIES) or (a == 1 and j == PIECES - 1):
+            if j == PIECES - 1 and a % 2 == 1:
                 nc.vector.tensor_copy(out=out_tile[:], in_=in_psum["kv", a, j][:])
             else:
                 nc.scalar.copy(out=out_tile[:], in_=in_psum["kv", a, j][:])
@@ -296,10 +293,10 @@ def tile_multiheadlatentattention_pa_kernel(tc, x, Wkv_a, kv_norm_w, Wkv_b, out_
                 in_=out_tile[:],
             )
 
-        def kv(tiles, j):
-            for a in tiles:
+        def kv(products):
+            for a, j in products:
                 second_matmul(a, j)
-            for a in tiles:
+            for a, j in products:
                 store_kv(a, j)
 
         pairs = raw_rope[:].rearrange("p (b h) (i e) -> p b (h i) e", b=2, e=2)
@@ -330,75 +327,71 @@ def tile_multiheadlatentattention_pa_kernel(tc, x, Wkv_a, kv_norm_w, Wkv_b, out_
                 in_=k_rope[:].rearrange("p b (h i) e -> p (b h) (i e)", h=SEQ_HALVES),
             )
 
+        transpose_x(0, nc.scalar.copy)
+        transpose_x(1, nc.scalar.copy)
+        quantise_x(0)
         regroup_wa(0)
-        rope_tables_scalar()
+        quantise_x(1)
         for g in range(PASSES):
             if g + 1 < PASSES:
                 regroup_wa(g + 1)
             if g == PASSES - 2:
                 spread_gain()
-            quantise_wa(g)
-
-        transpose_x(0)
-        transpose_x(1)
+            quantise_wa(g, 0, LATENT)
+        rope_tables_scalar()
         load_sqrt_table()
-        quantise_x(0)
-        quantise_x(1)
-        latent(0)
-        latent(1)
-        regroup_wb(0)
-        quantise_wb(0)
-        normalise(0)
-        regroup_wb(1)
-        normalise(1)
-        transpose_x(2)
-        transpose_n(0, nc.scalar.copy)
-        transpose_x(3)
-        rope_key(0)
-        rope_key(1)
-        quantise_n(0)
+
+        transpose_x(2, nc.vector.tensor_copy)
+        transpose_x(3, nc.scalar.copy)
         quantise_x(2)
-        transpose_n(1, nc.vector.tensor_copy)
-        quantise_n(1)
+        regroup_wb(0)
         quantise_x(3)
-        quantise_wb(1)
-        regroup_wb(2)
-        quantise_wb(2)
 
-        kv((0,), 0)
-        latent(2)
-        kv((1,), 0)
-        latent(3)
-        kv((0, 1), 1)
+        for a in range(TILES):
+            latent(a)
+        normalise(0)
+        quantise_wb(0)
+        normalise(1)
+        regroup_wb(1)
         normalise(2)
-        rope_key(2)
-        rope_key(3)
-        rope_by_cos()
-        normalise(3)
-        rope_by_sin()
-        second_matmul(0, 2)
-        second_matmul(1, 2)
-        transpose_n(2, nc.scalar.copy)
-        store_kv(0, 2)
-        transpose_n(3, nc.scalar.copy)
-        store_kv(1, 2)
+        quantise_wb(1)
+        for a in range(TILES - 1):
+            transpose_n(a, nc.scalar.copy)
+        quantise_n(0)
+        quantise_n(1)
+        regroup_wb(2)
         quantise_n(2)
-        rope_sum()
+        normalise(3)
+        quantise_wb(2)
         regroup_wb(3)
-        quantise_n(3)
-        for a in (2, 3):
-            for j in range(3):
-                second_matmul(a, j)
-        for a in (2, 3):
-            for j in range(3):
-                store_kv(a, j)
 
+        early = ((0, 0), (1, 0), (0, 1), (1, 1), (2, 0), (2, 1))
+        for a, j in early:
+            second_matmul(a, j)
+        transpose_n(TILES - 1, nc.vector.tensor_copy)
+        quantise_n(TILES - 1)
+        for a, j in early:
+            store_kv(a, j)
         quantise_wb(3)
-        for j in range(4, PIECES - 1):
+        regroup_wb(4)
+        quantise_wb(4)
+        kv(((0, 2), (1, 2), (2, 2)))
+        kv(((3, 0), (3, 1), (3, 2)))
+
+        for g in range(PASSES):
+            quantise_wa(g, LATENT, A_COLS)
+        for j in range(5, PIECES - 1):
             regroup_wb(j)
             quantise_wb(j)
         regroup_wb(PIECES - 1)
+
         for j in range(3, PIECES):
-            if j == PIECES - 2:
-                quantise_wb(PIECES - 1)
-            kv(range(TILES), j)
+            if j == 5:
+                for a in range(TILES):
+                    rope_key(a)
+            if j == PIECES - 1:
+                rope_by_cos()
+                rope_by_sin()
+                rope_sum()
+                quantise_wb(j)
+            kv([(a, j) for a in range(TILES)])

from contextlib import ExitStack

import concourse.mybir as mybir
from concourse.masks import make_identity

F32 = mybir.dt.float32
BF16 = mybir.dt.bfloat16
I32 = mybir.dt.int32
U32 = mybir.dt.uint32
U8 = mybir.dt.uint8
FP8X4 = mybir.dt.float8_e4m3fn_x4
ALU = mybir.AluOpType
ACT = mybir.ActivationFunctionType

P = 128
PACK = 4
K_PASS = P * PACK
TOKENS = 512
TILES = TOKENS // P
SEQ_HALVES = 2
D_MODEL = 2048
PASSES = D_MODEL // K_PASS
LATENT = 512
ROPE = 128
ROPE_PAIRS = ROPE // 2
A_COLS = LATENT + ROPE
KV_COLS = 4096
HEAD_DIM = 128
CHUNK_COLS = 1024
CHUNK_HEADS = CHUNK_COLS // (2 * HEAD_DIM)
CHUNKS = KV_COLS // CHUNK_COLS
PIECE_COLS = CHUNK_HEADS * HEAD_DIM
PIECES = 2 * CHUNKS
RMS_EPS = 1.1920928955078125e-07
ROPE_BASE = 10000.0
TWO_PI = 6.283185307179586

FLOPS = 2 * TOKENS * D_MODEL * A_COLS + 2 * TOKENS * LATENT * KV_COLS

WA_VECTOR_COLS = 320
RUN = 4


def tile_multiheadlatentattention_pa_kernel(tc, x, Wkv_a, kv_norm_w, Wkv_b, out_0, out_1, out_2):
    nc = tc.nc
    x_rows = x.flatten_outer_dims()
    kv_out = [
        out_0.rearrange("b s h d -> (b s) (h d)"),
        out_1.rearrange("b s h d -> (b s) (h d)"),
    ]
    with ExitStack() as ctx:
        keep = ctx.enter_context(tc.tile_pool(name="keep", bufs=1))
        regrouped = ctx.enter_context(tc.tile_pool(name="regrouped", bufs=3))
        scrap = ctx.enter_context(tc.tile_pool(name="scrap", bufs=2))
        leaving = ctx.enter_context(tc.tile_pool(name="leaving", bufs=12))
        banks = ctx.enter_context(tc.psum_pool(name="banks", bufs=7))
        rope_bank = ctx.enter_context(tc.psum_pool(name="rope_bank", bufs=1))
        ctx.enter_context(tc.manual_schedule())

        wa_raw = [keep.tile([P, PACK, A_COLS], BF16, name="wa_raw%d" % g) for g in range(PASSES)]
        wa_grouped = [
            keep.tile([P, A_COLS, PACK], BF16, name="wa_grouped%d" % g, align_bytes=64) for g in range(PASSES)
        ]
        wa_codes = keep.tile([P, PASSES, A_COLS], U32, name="wa_codes", align_bytes=64)
        wa_scales = keep.tile([P, PASSES, A_COLS], U8, name="wa_scales", align_bytes=64)
        x_raw = [keep.tile([P, D_MODEL], BF16, name="x_raw%d" % a) for a in range(TILES)]
        x_grouped = [keep.tile([P, PASSES, P, 2], F32, name="x_grouped%d" % a, align_bytes=64) for a in range(TILES)]
        x_codes = [keep.tile([P, PASSES * P], U32, name="x_codes%d" % a, align_bytes=64) for a in range(TILES)]
        x_scales = [keep.tile([P, PASSES * P], U8, name="x_scales%d" % a, align_bytes=64) for a in range(TILES)]
        sum_squares = [keep.tile([P, 1], F32, name="sum_squares%d" % a) for a in range(TILES)]
        rms = [keep.tile([P, 1], F32, name="rms%d" % a) for a in range(TILES)]
        inv_rms = [keep.tile([P, 1], F32, name="inv_rms%d" % a) for a in range(TILES)]
        normed = [keep.tile([P, LATENT], BF16, name="normed%d" % a) for a in range(TILES)]
        n_grouped = [keep.tile([P, P, PACK], BF16, name="n_grouped%d" % a, align_bytes=64) for a in range(TILES)]
        n_codes = [keep.tile([P, P], U32, name="n_codes%d" % a, align_bytes=64) for a in range(TILES)]
        n_scales = [keep.tile([P, P], U8, name="n_scales%d" % a, align_bytes=64) for a in range(TILES)]
        wb_raw = [keep.tile([P, PACK, CHUNK_COLS], BF16, name="wb_raw%d" % c) for c in range(CHUNKS)]
        wb_codes = keep.tile([P, PIECES, PIECE_COLS], U32, name="wb_codes", align_bytes=64)
        wb_scales = keep.tile([P, PIECES, PIECE_COLS], U8, name="wb_scales", align_bytes=64)
        raw_rope = rope_bank.tile([P, TILES, ROPE], F32, name="raw_rope")
        in_psum = {}
        wb_grouped = {}

        eps = keep.tile([P, 1], F32, name="eps")
        nc.vector.memset(eps[:], RMS_EPS)
        table_loaded = keep.tile([P, 2], F32, name="table_loaded")
        nc.scalar.activation(out=table_loaded[:, 0:1], in_=eps[:], func=ACT.Sin)
        gain_row = keep.tile([P, LATENT], BF16, name="gain_row")
        nc.vector.memset(gain_row[:], 0.0)
        position_int = keep.tile([P, SEQ_HALVES], I32, name="position_int")
        nc.gpsimd.iota(position_int[:], pattern=[[P, SEQ_HALVES]], base=0, channel_multiplier=1)

        def load_wa(g):
            nc.sync.dma_start(
                out=wa_raw[g][:].rearrange("p (u e) c -> p u (e c)", u=2, e=2),
                in_=Wkv_a[K_PASS * g : K_PASS * (g + 1), :].rearrange("(u p e) c -> p u (e c)", u=2, p=P, e=2),
            )

        def load_x(a):
            nc.sync.dma_start(out=x_raw[a][:], in_=x_rows[P * a : P * (a + 1), :])

        def load_wb(c):
            nc.sync.dma_start(
                out=wb_raw[c][:],
                in_=Wkv_b[:, CHUNK_COLS * c : CHUNK_COLS * (c + 1)].rearrange("(t p) n -> p t n", t=PACK, p=P),
            )

        load_x(0)
        load_x(1)
        for g in range(PASSES):
            load_wa(g)
        nc.sync.dma_start(out=gain_row[0:1, :], in_=kv_norm_w.rearrange("(o n) -> o n", o=1))
        load_x(2)
        load_x(3)
        for c in range(CHUNKS):
            load_wb(c)

        frequency = keep.tile([P, ROPE_PAIRS], F32, name="frequency")
        nc.vector.memset(frequency[:, 0:1], 1.0)
        for filled in (1, 2, 4, 8, 16, 32):
            nc.vector.tensor_scalar_mul(
                out=frequency[:, filled : 2 * filled],
                in0=frequency[:, 0:filled],
                scalar1=ROPE_BASE ** (-2.0 * filled / ROPE),
            )
        position = keep.tile([P, SEQ_HALVES], F32, name="position")
        nc.vector.tensor_copy(out=position[:], in_=position_int[:])
        turns = keep.tile([P, 2, SEQ_HALVES, ROPE_PAIRS], F32, name="turns")
        for half in range(SEQ_HALVES):
            nc.vector.tensor_scalar(
                out=turns[:, 0, half, :],
                in0=frequency[:],
                scalar1=position[:, half : half + 1],
                scalar2=1.0 / TWO_PI,
                op0=ALU.mult,
                op1=ALU.mult,
            )
        nc.vector.tensor_scalar_add(out=turns[:, 1, :, :], in0=turns[:, 0, :, :], scalar1=0.25)
        turns_row = turns[:].rearrange("p s h i -> p (s h i)")
        whole_int = keep.tile([P, 2 * P], I32, name="whole_int")
        nc.vector.tensor_copy(out=whole_int[:], in_=turns_row)
        whole = keep.tile([P, 2 * P], F32, name="whole")
        nc.vector.tensor_copy(out=whole[:], in_=whole_int[:])
        part_turn = keep.tile([P, 2 * P], F32, name="part_turn")
        nc.vector.tensor_tensor(out=part_turn[:], in0=turns_row, in1=whole[:], op=ALU.subtract)
        SIN, COS, MINUS_SIN = 0, 1, 2
        trig = keep.tile([P, 3, SEQ_HALVES * ROPE_PAIRS], F32, name="trig")

        ones = keep.tile([P, P], BF16, name="ones")
        nc.vector.memset(ones[:], 1.0)
        identity_f32 = keep.tile([P, P], F32, name="identity_f32")
        make_identity(nc, identity_f32[:])
        identity_bf16 = keep.tile([P, P], BF16, name="identity_bf16")
        make_identity(nc, identity_bf16[:])
        gain = keep.tile([P, LATENT], F32, name="gain")

        def rope_tables_scalar():
            nc.scalar.activation(
                out=trig[:, SIN : COS + 1, :].rearrange("p s n -> p (s n)"), in_=part_turn[:], func=ACT.Sin, scale=TWO_PI
            )
            nc.scalar.activation(out=trig[:, MINUS_SIN, :], in_=part_turn[:, 0:P], func=ACT.Sin, scale=-TWO_PI)

        def load_sqrt_table():
            nc.scalar.activation(out=table_loaded[:, 1:2], in_=eps[:], func=ACT.Sqrt)

        def regroup_wa(g):
            for copy, first, last in (
                (nc.scalar.copy, WA_VECTOR_COLS, A_COLS),
                (nc.vector.tensor_copy, 0, WA_VECTOR_COLS),
            ):
                copy(
                    out=wa_grouped[g][:, first:last, :].rearrange("p (c i) t -> p c t i", i=RUN),
                    in_=wa_raw[g][:, :, first:last].rearrange("p t (c i) -> p c t i", i=RUN),
                )

        def quantise_wa(g, first, last):
            nc.vector.quantize_mx(
                out=wa_codes[:, g, first:last].bitcast(FP8X4),
                scales=wa_scales[:, g, first:last],
                in_=wa_grouped[g][:, first:last, :].rearrange("p c t -> p (c t)"),
            )

        def spread_gain():
            summed = banks.tile([P, LATENT], F32, name="summed", tag="bank")
            nc.tensor.matmul(out=summed[:], lhsT=ones[:], rhs=gain_row[:], start=True, stop=True)
            nc.vector.tensor_copy(out=gain[:], in_=summed[:])

        def transpose_x(a, copy):
            words = x_raw[a][:].bitcast(F32)
            for first_pass in range(0, PASSES, 2):
                turned = banks.tile([P, 2, 2, P], F32, name="turned", tag="bank")
                for g in range(2):
                    for u in range(2):
                        first_word = 2 * P * (first_pass + g) + P * u
                        nc.tensor.transpose(turned[:, g, u, :], words[:, first_word : first_word + P], identity_f32[:])
                copy(
                    out=x_grouped[a][:, first_pass : first_pass + 2, :, :],
                    in_=turned[:].rearrange("p g u r -> p g r u"),
                )

        def quantise_x(a):
            for first_pass in range(0, PASSES, 2):
                columns = slice(P * first_pass, P * (first_pass + 2))
                nc.vector.quantize_mx(
                    out=x_codes[a][:, columns].bitcast(FP8X4),
                    scales=x_scales[a][:, columns],
                    in_=x_grouped[a][:, first_pass : first_pass + 2, :, :].rearrange("p g r u -> p (g r u)").bitcast(BF16),
                )

        def first_matmul(a, out, first, last):
            for g in range(PASSES):
                nc.tensor.matmul_mx(
                    out=out,
                    lhsT=x_codes[a][:, P * g : P * (g + 1)].bitcast(FP8X4),
                    lhsT_scale=x_scales[a][:, P * g : P * (g + 1)],
                    rhs=wa_codes[:, g, first:last].bitcast(FP8X4),
                    rhs_scale=wa_scales[:, g, first:last],
                    start=(g == 0),
                    stop=(g == PASSES - 1),
                )

        def latent(a):
            in_psum["latent", a] = banks.tile([P, LATENT], F32, name="latent", tag="bank")
            first_matmul(a, in_psum["latent", a][:], 0, LATENT)
            squares = scrap.tile([P, LATENT], BF16, name="squares")
            nc.scalar.activation(out=squares[:], in_=in_psum["latent", a][:], func=ACT.Square, accum_out=sum_squares[a][:])
            nc.scalar.activation(out=rms[a][:], in_=sum_squares[a][:], func=ACT.Sqrt, scale=1.0 / LATENT, bias=eps[:])

        def rope_key(a):
            first_matmul(a, raw_rope[:, a, :], LATENT, A_COLS)

        def normalise(a):
            nc.vector.reciprocal(out=inv_rms[a][:], in_=rms[a][:])
            nc.vector.scalar_tensor_tensor(
                out=normed[a][:],
                in0=in_psum["latent", a][:],
                scalar=inv_rms[a][:],
                in1=gain[:],
                op0=ALU.mult,
                op1=ALU.mult,
            )

        def transpose_n(a, copy):
            turned = banks.tile([P, PACK, P], BF16, name="turned_n", tag="bank")
            for t in range(PACK):
                nc.tensor.transpose(turned[:, t, :], normed[a][:, P * t : P * (t + 1)], identity_bf16[:])
            copy(out=n_grouped[a][:], in_=turned[:].rearrange("p t r -> p r t"))

        def quantise_n(a):
            nc.vector.quantize_mx(
                out=n_codes[a][:].bitcast(FP8X4),
                scales=n_scales[a][:],
                in_=n_grouped[a][:].rearrange("p r t -> p (r t)"),
            )

        def regroup_wb(j):
            wb_grouped[j] = regrouped.tile([P, PIECE_COLS, PACK], BF16, name="wb_grouped", align_bytes=64)
            by_head = wb_raw[j // 2][:].rearrange(
                "p t (h k c i) -> p t h k c i", h=CHUNK_HEADS, k=2, c=HEAD_DIM // RUN, i=RUN
            )
            nc.vector.tensor_copy(
                out=wb_grouped[j][:].rearrange("p (h c i) t -> p h c t i", h=CHUNK_HEADS, c=HEAD_DIM // RUN, i=RUN),
                in_=by_head[:, :, :, j % 2, :, :].rearrange("p t h c i -> p h c t i"),
            )

        def quantise_wb(j):
            nc.vector.quantize_mx(
                out=wb_codes[:, j, :].bitcast(FP8X4),
                scales=wb_scales[:, j, :],
                in_=wb_grouped[j][:].rearrange("p c t -> p (c t)"),
            )

        def second_matmul(a, j):
            in_psum["kv", a, j] = banks.tile([P, PIECE_COLS], F32, name="kv", tag="bank")
            nc.tensor.matmul_mx(
                out=in_psum["kv", a, j][:],
                lhsT=n_codes[a][:].bitcast(FP8X4),
                lhsT_scale=n_scales[a][:],
                rhs=wb_codes[:, j, :].bitcast(FP8X4),
                rhs_scale=wb_scales[:, j, :],
                start=True,
                stop=True,
            )

        def store_kv(a, j):
            out_tile = leaving.tile([P, PIECE_COLS], F32, name="out_tile")
            if j == PIECES - 1 and a % 2 == 1:
                nc.vector.tensor_copy(out=out_tile[:], in_=in_psum["kv", a, j][:])
            else:
                nc.scalar.copy(out=out_tile[:], in_=in_psum["kv", a, j][:])
            nc.sync.dma_start(
                out=kv_out[j % 2][P * a : P * (a + 1), PIECE_COLS * (j // 2) : PIECE_COLS * (j // 2 + 1)],
                in_=out_tile[:],
            )

        def kv(products):
            for a, j in products:
                second_matmul(a, j)
            for a, j in products:
                store_kv(a, j)

        pairs = raw_rope[:].rearrange("p (b h) (i e) -> p b (h i) e", b=2, e=2)
        both = [P, 2, P]
        by_cos = keep.tile([P, 2, P, 2], F32, name="by_cos")
        by_sin = keep.tile([P, 2, 2, P], F32, name="by_sin")
        k_rope = keep.tile([P, 2, P, 2], F32, name="k_rope")

        def rope_by_cos():
            nc.vector.tensor_tensor(
                out=by_cos[:], in0=pairs, in1=trig[:, COS, :].unsqueeze(1).unsqueeze(3).to_broadcast([P, 2, P, 2]), op=ALU.mult
            )

        def rope_by_sin():
            nc.vector.tensor_tensor(
                out=by_sin[:, 0, :, :], in0=pairs[:, :, :, 1], in1=trig[:, MINUS_SIN, :].unsqueeze(1).to_broadcast(both), op=ALU.mult
            )
            nc.vector.tensor_tensor(
                out=by_sin[:, 1, :, :], in0=pairs[:, :, :, 0], in1=trig[:, SIN, :].unsqueeze(1).to_broadcast(both), op=ALU.mult
            )

        def rope_sum():
            nc.vector.tensor_tensor(
                out=k_rope[:], in0=by_cos[:], in1=by_sin[:].rearrange("p e b n -> p b n e"), op=ALU.add
            )
            nc.sync.dma_start(
                out=out_2.rearrange("b (h p) o d -> p (b h) (o d)", h=SEQ_HALVES, p=P),
                in_=k_rope[:].rearrange("p b (h i) e -> p (b h) (i e)", h=SEQ_HALVES),
            )

        transpose_x(0, nc.scalar.copy)
        transpose_x(1, nc.scalar.copy)
        quantise_x(0)
        regroup_wa(0)
        quantise_x(1)
        for g in range(PASSES):
            if g + 1 < PASSES:
                regroup_wa(g + 1)
            if g == PASSES - 2:
                spread_gain()
            quantise_wa(g, 0, LATENT)
        rope_tables_scalar()
        load_sqrt_table()

        transpose_x(2, nc.vector.tensor_copy)
        transpose_x(3, nc.scalar.copy)
        quantise_x(2)
        regroup_wb(0)
        quantise_x(3)

        for a in range(TILES):
            latent(a)
        normalise(0)
        quantise_wb(0)
        normalise(1)
        regroup_wb(1)
        normalise(2)
        quantise_wb(1)
        for a in range(TILES - 1):
            transpose_n(a, nc.scalar.copy)
        quantise_n(0)
        quantise_n(1)
        regroup_wb(2)
        quantise_n(2)
        normalise(3)
        quantise_wb(2)
        regroup_wb(3)

        early = ((0, 0), (1, 0), (0, 1), (1, 1), (2, 0), (2, 1))
        for a, j in early:
            second_matmul(a, j)
        transpose_n(TILES - 1, nc.vector.tensor_copy)
        quantise_n(TILES - 1)
        for a, j in early:
            store_kv(a, j)
        quantise_wb(3)
        regroup_wb(4)
        quantise_wb(4)
        kv(((0, 2), (1, 2), (2, 2)))
        kv(((3, 0), (3, 1), (3, 2)))

        for g in range(PASSES):
            quantise_wa(g, LATENT, A_COLS)
        for j in range(5, PIECES - 1):
            regroup_wb(j)
            quantise_wb(j)
        regroup_wb(PIECES - 1)

        for j in range(3, PIECES):
            if j == 5:
                for a in range(TILES):
                    rope_key(a)
            if j == PIECES - 1:
                rope_by_cos()
                rope_by_sin()
                rope_sum()
                quantise_wb(j)
            kv([(a, j) for a in range(TILES)])
